import numpy as np
import ml_dtypes


def mxq(x, axis, fmt="e4m3"):
    dtype, down = {"e4m3": (ml_dtypes.float8_e4m3fn, 7), "e5m2": (ml_dtypes.float8_e5m2, 14)}[fmt]
    v = np.moveaxis(np.asarray(x, np.float32).astype(ml_dtypes.bfloat16).astype(np.float64), axis, -1)
    blocks = v.reshape(v.shape[:-1] + (-1, 32))
    amax = np.abs(blocks).max(-1, keepdims=True)
    byte = np.maximum(np.where(amax > 0, np.frexp(amax)[1] - 1 + 127, 0) - down, 1)
    scale = np.exp2(byte - 127.0)
    codes = (blocks / scale).astype(np.float32).astype(dtype).astype(np.float64)
    return np.moveaxis((codes * scale).reshape(v.shape), -1, axis)


WIDE = False


def mx_kscale(k):
    if not WIDE:
        return np.ones(k)
    levels = np.array([10, -10, 5, -5, 0])
    a = np.random.permutation(np.resize(levels, k // 512 * 4)).reshape(k // 512, 4)
    idx = np.arange(k)
    return np.exp2(a[idx // 512, idx % 128 // 32])


BF16 = ml_dtypes.bfloat16


def bf(x):
    return np.asarray(x, np.float32).astype(BF16)


def f64(x):
    return np.asarray(x).astype(np.float64)


B, LQ, LA, CTX, E, C = 24, 128, 512, 4, 128, 256
PAD = CTX // 2
K = CTX * E


def _windows(x):
    Bx, L, Ed = x.shape
    xp = np.pad(x, ((0, 0), (PAD, PAD), (0, 0)))
    w = np.stack([xp[:, j:j + L] for j in range(CTX)], axis=2)
    return w.reshape(Bx, L, CTX * Ed)


def setup_inputs():
    s = mx_kscale(K)[:E]
    sk = np.tile(s, CTX)
    return {"question": bf(np.random.standard_normal((B, LQ, E)) * s),
            "answer": bf(np.random.standard_normal((B, LA, E)) * s),
            "W": bf(np.random.uniform(-1.0, 1.0, (K, C)) / np.sqrt(K) / sk[:, None]),
            "b": bf(np.random.uniform(-1.0, 1.0, C) * 0.5)}


def reference(question, answer, W, b):
    Wq = mxq(f64(W), 0, "e4m3")
    q = _windows(f64(question))
    a = _windows(f64(answer))
    Q = (mxq(q, 2, "e4m3") @ Wq).transpose(0, 2, 1) + f64(b)[None, :, None]
    A = (mxq(a, 2, "e4m3") @ Wq).transpose(0, 2, 1) + f64(b)[None, :, None]
    return (Q, A)

@@ -1,0 +1,252 @@
+from contextlib import ExitStack
+
+import concourse.mybir as mybir
+from concourse.masks import make_identity
+
+FLOPS = 2 * 24 * (128 + 512) * 512 * 256
+
+F32 = mybir.dt.float32
+BF16 = mybir.dt.bfloat16
+I32 = mybir.dt.int32
+U32 = mybir.dt.uint32
+U8 = mybir.dt.uint8
+FP8X4 = mybir.dt.float8_e4m3fn_x4
+IDENTITY = mybir.ActivationFunctionType.Identity
+
+P = 128
+NSET = 6
+A_COLS = 512
+A_PITCH = 576
+Q_COLS = 128
+Q_PITCH = 192
+
+
+def tile_qa_cnn_t_kernel(tc, question, answer, W, b, out_0, out_1):
+    nc = tc.nc
+    with ExitStack() as ctx:
+        keep = ctx.enter_context(tc.tile_pool(name="keep", bufs=1))
+        gpool = ctx.enter_context(tc.tile_pool(name="grouped", bufs=3))
+        opool = ctx.enter_context(tc.tile_pool(name="outs", bufs=4))
+        tp_ps = ctx.enter_context(tc.psum_pool(name="tp", bufs=2))
+        mm_ps = ctx.enter_context(tc.psum_pool(name="mm", bufs=6))
+
+        w_raw = keep.tile([P, 1024], BF16, name="w_raw")
+        nc.sync.dma_start(out=w_raw[:], in_=W.rearrange("(p t) c -> p (t c)", t=4))
+        b_bf = keep.tile([P, 2], BF16, name="b_bf")
+        with nc.allow_non_contiguous_dma(reason="256 bias values, one to a partition"):
+            nc.scalar.dma_start(out=b_bf[:], in_=b.rearrange("(h c) -> c h", h=2))
+        a_rows = answer.flatten_outer_dims().rearrange(
+            "(n b w g) e -> n w b (g e)", n=NSET, b=4, g=4
+        )
+        xa = []
+        for n in range(NSET):
+            x = keep.tile([P, 4, 512], BF16, name="xa%d" % n)
+            nc.sync.dma_start(out=x[:], in_=a_rows[n])
+            xa.append(x)
+        xq = keep.tile([P, NSET, 512], BF16, name="xq")
+        nc.sync.dma_start(
+            out=xq[:],
+            in_=question.flatten_outer_dims().rearrange("(n k g) e -> k n (g e)", n=NSET, g=4),
+        )
+
+        ident = keep.tile([P, P], F32, name="ident")
+        make_identity(nc, ident[:])
+        ident_b = keep.tile([P, P], BF16, name="ident_b")
+        make_identity(nc, ident_b[:])
+        twice = keep.tile([P, 2 * P], BF16, name="twice")
+        nc.vector.tensor_copy(out=twice[:, 0:P], in_=ident_b[:])
+        nc.vector.tensor_copy(out=twice[:, P : 2 * P], in_=ident_b[:])
+        bias = keep.tile([P, 2], F32, name="bias")
+        nc.vector.tensor_copy(out=bias[:], in_=b_bf[:])
+
+        c0_a = keep.tile([P, 7 * A_PITCH], U32, name="c0_a", align_bytes=64)
+        s0_a = keep.tile([P, 7 * A_PITCH], U8, name="s0_a", align_bytes=64)
+        c0_q = keep.tile([P, 7 * Q_PITCH], U32, name="c0_q", align_bytes=64)
+        s0_q = keep.tile([P, 7 * Q_PITCH], U8, name="s0_q", align_bytes=64)
+        c0_a_i = c0_a[:].bitcast(I32)
+        s0_a_i = s0_a[:].bitcast(I32)
+        c0_q_i = c0_q[:].bitcast(I32)
+        s0_q_i = s0_q[:].bitcast(I32)
+        nc.vector.memset(c0_a_i.rearrange("p (n c) -> p n c", c=A_PITCH)[:, :, 0:64], 0)
+        nc.vector.memset(c0_q_i.rearrange("p (n c) -> p n c", c=Q_PITCH)[:, :, 0:64], 0)
+        nc.vector.memset(s0_a_i, 0)
+        nc.vector.memset(s0_q_i, 0)
+        cs_a = {}
+        ss_a = {}
+        cs_q = {}
+        ss_q = {}
+        for s in (0, 1, 3):
+            cs_a[s] = keep.tile([P, NSET * A_COLS], U32, name="cs_a%d" % s, align_bytes=64)
+            ss_a[s] = keep.tile([P, NSET * A_COLS], U8, name="ss_a%d" % s, align_bytes=64)
+            cs_q[s] = keep.tile([P, NSET * Q_COLS], U32, name="cs_q%d" % s, align_bytes=64)
+            ss_q[s] = keep.tile([P, NSET * Q_COLS], U8, name="ss_q%d" % s, align_bytes=64)
+
+        w_view = w_raw[:].rearrange("p (t c) -> p t c", t=4)
+        w_grp = keep.tile([P, 4, 2, P, 4], BF16, name="w_grp", align_bytes=64)
+        wq = keep.tile([P, 4, 256], U32, name="wq", align_bytes=64)
+        wqs = keep.tile([P, 4, 256], U8, name="wqs", align_bytes=64)
+        for s in (2, 1, 0, 3):
+            rot = (2 - s) % 4
+            for h in range(2):
+                ps = mm_ps.tile([P, 4, P], F32, tag="mm")
+                nc.tensor.matmul(
+                    out=ps[:],
+                    lhsT=twice[:, 32 * rot : 32 * rot + P],
+                    rhs=w_view[:, :, P * h : P * h + P],
+                    start=True,
+                    stop=True,
+                )
+                nc.scalar.copy(out=w_grp[:, s, h], in_=ps[:].rearrange("p t c -> p c t"))
+            nc.vector.quantize_mx(
+                out=wq[:, s, :].bitcast(FP8X4),
+                scales=wqs[:, s, :],
+                in_=w_grp[:, s].rearrange("p h c t -> p (h c t)"),
+            )
+
+        def spread(src_c, src_s, dst_c, dst_s):
+            for src, dst in ((src_c, dst_c), (src_s, dst_s)):
+                nc.vector.tensor_copy(out=dst[1][0:96], in_=src(0)[0:96])
+                nc.vector.tensor_copy(out=dst[1][96:128], in_=src(-1)[96:128])
+                nc.vector.tensor_copy(out=dst[0][0:64], in_=src(0)[0:64])
+                nc.vector.tensor_copy(out=dst[0][64:128], in_=src(-1)[64:128])
+                nc.vector.tensor_copy(out=dst[3], in_=src(0))
+                nc.vector.tensor_copy(out=dst[3][0:32], in_=src(1)[0:32])
+
+        def prep_a(n):
+            xw = xa[n][:].bitcast(F32)
+            grouped = gpool.tile([P, 4 * A_COLS], BF16, tag="ga", align_bytes=64)
+            g32 = grouped[:].bitcast(F32).rearrange("p (w b u) -> p w b u", b=4, u=2)
+            for half in range(2):
+                tp = tp_ps.tile([P, 2, 2, P], F32, tag="tp")
+                for bb in range(2):
+                    for u in range(2):
+                        nc.tensor.transpose(
+                            tp[:, bb, u, :],
+                            xw[:, 2 * half + bb, :].rearrange("p (m u) -> p u m", u=2)[:, u, :],
+                            ident[:],
+                        )
+                nc.vector.tensor_copy(
+                    out=g32[:, :, 2 * half : 2 * half + 2, :],
+                    in_=tp[:].rearrange("p b u w -> p w b u"),
+                )
+            base = 64 + A_PITCH * n
+            nc.vector.quantize_mx(
+                out=c0_a[:, base : base + A_COLS].bitcast(FP8X4),
+                scales=s0_a[:, base : base + A_COLS],
+                in_=grouped[:],
+            )
+            spread(
+                lambda d: c0_a_i[:, base + 4 * d : base + 4 * d + A_COLS],
+                lambda d: s0_a_i[:, base // 4 + d : base // 4 + d + A_COLS // 4],
+                dict((s, cs_a[s][:].bitcast(I32)[:, A_COLS * n : A_COLS * (n + 1)]) for s in (0, 1, 3)),
+                dict(
+                    (s, ss_a[s][:].bitcast(I32)[:, A_COLS // 4 * n : A_COLS // 4 * (n + 1)])
+                    for s in (0, 1, 3)
+                ),
+            )
+
+        def prep_q():
+            xw = xq[:].bitcast(F32)
+            for pair in range(NSET // 2):
+                grouped = gpool.tile([P, 2, 4 * Q_COLS], BF16, tag="gq", align_bytes=64)
+                g32 = grouped[:].bitcast(F32)
+                tp = tp_ps.tile([P, 2, 2, P], F32, tag="tp")
+                for bb in range(2):
+                    for u in range(2):
+                        nc.tensor.transpose(
+                            tp[:, bb, u, :],
+                            xw[:, 2 * pair + bb, :].rearrange("p (m u) -> p u m", u=2)[:, u, :],
+                            ident[:],
+                        )
+                for bb in range(2):
+                    nc.vector.tensor_copy(
+                        out=g32[:, bb, :].rearrange("p (w b u) -> p w b u", b=4, u=2),
+                        in_=tp[:, bb, :, :].rearrange("p u (b w) -> p w b u", b=4),
+                    )
+                for bb in range(2):
+                    base = 64 + Q_PITCH * (2 * pair + bb)
+                    nc.vector.quantize_mx(
+                        out=c0_q[:, base : base + Q_COLS].bitcast(FP8X4),
+                        scales=s0_q[:, base : base + Q_COLS],
+                        in_=grouped[:, bb, :],
+                    )
+            spread(
+                lambda d: c0_q_i[:, 64 + 4 * d : 64 + 4 * d + NSET * Q_PITCH].rearrange(
+                    "p (n c) -> p n c", c=Q_PITCH
+                )[:, :, 0:Q_COLS],
+                lambda d: s0_q_i[:, 16 + d : 16 + d + NSET * Q_PITCH // 4].rearrange(
+                    "p (n c) -> p n c", c=Q_PITCH // 4
+                )[:, :, 0 : Q_COLS // 4],
+                dict(
+                    (s, cs_q[s][:].bitcast(I32).rearrange("p (n c) -> p n c", c=Q_COLS))
+                    for s in (0, 1, 3)
+                ),
+                dict(
+                    (s, ss_q[s][:].bitcast(I32).rearrange("p (n c) -> p n c", c=Q_COLS // 4))
+                    for s in (0, 1, 3)
+                ),
+            )
+
+        def bank(h, plain_c, plain_s, plain_at, moved_c, moved_s, moved_at, dest):
+            acc = mm_ps.tile([P, 4, P], F32, tag="mm")
+            for s in (2, 1, 0, 3):
+                if s == 2:
+                    codes, planes, at = plain_c, plain_s, plain_at
+                else:
+                    codes, planes, at = moved_c[s], moved_s[s], moved_at
+                nc.tensor.matmul_mx(
+                    out=acc[:, s, :],
+                    lhsT=wq[:, s, P * h : P * h + P].bitcast(FP8X4),
+                    lhsT_scale=wqs[:, s, P * h : P * h + P],
+                    rhs=codes[:, at : at + P].bitcast(FP8X4),
+                    rhs_scale=planes[:, at : at + P],
+                    start=True,
+                    stop=True,
+                )
+            nc.scalar.activation(
+                out=dest.rearrange("c b (u s) -> c b u s", s=4),
+                in_=acc[:].rearrange("c s (u b) -> c b u s", b=4),
+                func=IDENTITY,
+                bias=bias[:, h : h + 1],
+                scale=1.0,
+            )
+
+        def run_a(n):
+            for h in range(2):
+                o = opool.tile([P, 4, 512], F32, tag="oa")
+                for v in range(4):
+                    bank(
+                        h, c0_a, s0_a, 64 + A_PITCH * n + P * v,
+                        cs_a, ss_a, A_COLS * n + P * v,
+                        o[:, :, P * v : P * v + P],
+                    )
+                nc.sync.dma_start(
+                    out=out_1[4 * n : 4 * n + 4, P * h : P * h + P, :].rearrange("b c i -> c b i"),
+                    in_=o[:],
+                )
+
+        def run_q(pair):
+            for h in range(2):
+                o = opool.tile([P, 8, P], F32, tag="oq")
+                for bb in range(2):
+                    n = 2 * pair + bb
+                    bank(
+                        h, c0_q, s0_q, 64 + Q_PITCH * n,
+                        cs_q, ss_q, Q_COLS * n,
+                        o[:, 4 * bb : 4 * bb + 4, :],
+                    )
+                nc.sync.dma_start(
+                    out=out_0[8 * pair : 8 * pair + 8, P * h : P * h + P, :].rearrange("b c i -> c b i"),
+                    in_=o[:],
+                )
+
+        prep_a(0)
+        prep_a(1)
+        for n in range(NSET):
+            run_a(n)
+            if n + 2 < NSET:
+                prep_a(n + 2)
+            if n == NSET - 2:
+                prep_q()
+        for pair in range(NSET // 2):
+            run_q(pair)

@@ -204,8 +204,8 @@ def tile_qa_cnn_t_kernel(tc, question, answer, W, b, out_0, out_1):
                     stop=True,
                 )
             nc.scalar.activation(
-                out=dest.rearrange("c b (u s) -> c b u s", s=4),
-                in_=acc[:].rearrange("c s (u b) -> c b u s", b=4),
+                out=dest.rearrange("c b (u s) -> c u b s", s=4),
+                in_=acc[:].rearrange("c s (u b) -> c u b s", b=4),
                 func=IDENTITY,
                 bias=bias[:, h : h + 1],
                 scale=1.0,

@@ -12,6 +12,7 @@ U32 = mybir.dt.uint32
 U8 = mybir.dt.uint8
 FP8X4 = mybir.dt.float8_e4m3fn_x4
 IDENTITY = mybir.ActivationFunctionType.Identity
+ADD = mybir.AluOpType.add
 
 P = 128
 NSET = 6
@@ -19,6 +20,8 @@ A_COLS = 512
 A_PITCH = 576
 Q_COLS = 128
 Q_PITCH = 192
+MOVED = (0, 1, 3)
+VEC_EVERY = 5
 
 
 def tile_qa_cnn_t_kernel(tc, question, answer, W, b, out_0, out_1):
@@ -56,6 +59,11 @@ def tile_qa_cnn_t_kernel(tc, question, answer, W, b, out_0, out_1):
         twice = keep.tile([P, 2 * P], BF16, name="twice")
         nc.vector.tensor_copy(out=twice[:, 0:P], in_=ident_b[:])
         nc.vector.tensor_copy(out=twice[:, P : 2 * P], in_=ident_b[:])
+        perm = keep.tile([P, P], F32, name="perm")
+        nc.vector.tensor_copy(
+            out=perm[:].rearrange("p (w b) -> p w b", b=4),
+            in_=ident[:].rearrange("p (b w) -> p w b", b=4),
+        )
         bias = keep.tile([P, 2], F32, name="bias")
         nc.vector.tensor_copy(out=bias[:], in_=b_bf[:])
 
@@ -68,14 +76,14 @@ def tile_qa_cnn_t_kernel(tc, question, answer, W, b, out_0, out_1):
         c0_q_i = c0_q[:].bitcast(I32)
         s0_q_i = s0_q[:].bitcast(I32)
         nc.vector.memset(c0_a_i.rearrange("p (n c) -> p n c", c=A_PITCH)[:, :, 0:64], 0)
-        nc.vector.memset(c0_q_i.rearrange("p (n c) -> p n c", c=Q_PITCH)[:, :, 0:64], 0)
         nc.vector.memset(s0_a_i, 0)
+        nc.vector.memset(c0_q_i.rearrange("p (n c) -> p n c", c=Q_PITCH)[:, :, 0:64], 0)
         nc.vector.memset(s0_q_i, 0)
         cs_a = {}
         ss_a = {}
         cs_q = {}
         ss_q = {}
-        for s in (0, 1, 3):
+        for s in MOVED:
             cs_a[s] = keep.tile([P, NSET * A_COLS], U32, name="cs_a%d" % s, align_bytes=64)
             ss_a[s] = keep.tile([P, NSET * A_COLS], U8, name="ss_a%d" % s, align_bytes=64)
             cs_q[s] = keep.tile([P, NSET * Q_COLS], U32, name="cs_q%d" % s, align_bytes=64)
@@ -85,18 +93,26 @@ def tile_qa_cnn_t_kernel(tc, question, answer, W, b, out_0, out_1):
         w_grp = keep.tile([P, 4, 2, P, 4], BF16, name="w_grp", align_bytes=64)
         wq = keep.tile([P, 4, 256], U32, name="wq", align_bytes=64)
         wqs = keep.tile([P, 4, 256], U8, name="wqs", align_bytes=64)
-        for s in (2, 1, 0, 3):
-            rot = (2 - s) % 4
-            for h in range(2):
-                ps = mm_ps.tile([P, 4, P], F32, tag="mm")
-                nc.tensor.matmul(
-                    out=ps[:],
-                    lhsT=twice[:, 32 * rot : 32 * rot + P],
-                    rhs=w_view[:, :, P * h : P * h + P],
-                    start=True,
-                    stop=True,
-                )
-                nc.scalar.copy(out=w_grp[:, s, h], in_=ps[:].rearrange("p t c -> p c t"))
+
+        def prep_w():
+            nc.scalar.copy(
+                out=w_grp[:, 2].rearrange("p h c t -> p (h c) t"),
+                in_=w_view.rearrange("p t c -> p c t"),
+            )
+            for s in (0, 3, 1):
+                rot = (2 - s) % 4
+                for h in range(2):
+                    ps = mm_ps.tile([P, 4, P], F32, tag="mm")
+                    nc.tensor.matmul(
+                        out=ps[:],
+                        lhsT=twice[:, 32 * rot : 32 * rot + P],
+                        rhs=w_view[:, :, P * h : P * h + P],
+                        start=True,
+                        stop=True,
+                    )
+                    nc.scalar.copy(out=w_grp[:, s, h], in_=ps[:].rearrange("p t c -> p c t"))
+
+        def quant_w(s):
             nc.vector.quantize_mx(
                 out=wq[:, s, :].bitcast(FP8X4),
                 scales=wqs[:, s, :],
@@ -105,70 +121,97 @@ def tile_qa_cnn_t_kernel(tc, question, answer, W, b, out_0, out_1):
 
         def spread(src_c, src_s, dst_c, dst_s):
             for src, dst in ((src_c, dst_c), (src_s, dst_s)):
-                nc.vector.tensor_copy(out=dst[1][0:96], in_=src(0)[0:96])
-                nc.vector.tensor_copy(out=dst[1][96:128], in_=src(-1)[96:128])
+                nc.vector.tensor_copy(out=dst[3], in_=src(0))
                 nc.vector.tensor_copy(out=dst[0][0:64], in_=src(0)[0:64])
                 nc.vector.tensor_copy(out=dst[0][64:128], in_=src(-1)[64:128])
-                nc.vector.tensor_copy(out=dst[3], in_=src(0))
                 nc.vector.tensor_copy(out=dst[3][0:32], in_=src(1)[0:32])
+                nc.vector.tensor_copy(out=dst[1][0:96], in_=src(0)[0:96])
+                nc.vector.tensor_copy(out=dst[1][96:128], in_=src(-1)[96:128])
 
-        def prep_a(n):
-            xw = xa[n][:].bitcast(F32)
-            grouped = gpool.tile([P, 4 * A_COLS], BF16, tag="ga", align_bytes=64)
-            g32 = grouped[:].bitcast(F32).rearrange("p (w b u) -> p w b u", b=4, u=2)
-            for half in range(2):
-                tp = tp_ps.tile([P, 2, 2, P], F32, tag="tp")
-                for bb in range(2):
-                    for u in range(2):
-                        nc.tensor.transpose(
-                            tp[:, bb, u, :],
-                            xw[:, 2 * half + bb, :].rearrange("p (m u) -> p u m", u=2)[:, u, :],
-                            ident[:],
-                        )
-                nc.vector.tensor_copy(
-                    out=g32[:, :, 2 * half : 2 * half + 2, :],
-                    in_=tp[:].rearrange("p b u w -> p w b u"),
+        def prep_a(sets, between=None):
+            tiles = []
+            for n in sets:
+                xw = xa[n][:].bitcast(F32)
+                grouped = gpool.tile([P, 4 * A_COLS], BF16, tag="ga", align_bytes=64)
+                tiles.append(grouped)
+                g32 = grouped[:].bitcast(F32).rearrange("p (w b u) -> p w b u", b=4, u=2)
+                for half in range(2):
+                    tp = tp_ps.tile([P, 2, 2, P], F32, tag="tp")
+                    for bb in range(2):
+                        for u in range(2):
+                            nc.tensor.transpose(
+                                tp[:, bb, u, :],
+                                xw[:, 2 * half + bb, :].rearrange("p (m u) -> p u m", u=2)[:, u, :],
+                                ident[:],
+                            )
+                    nc.vector.tensor_copy(
+                        out=g32[:, :, 2 * half : 2 * half + 2, :],
+                        in_=tp[:].rearrange("p b u w -> p w b u"),
+                    )
+            if between is not None:
+                between()
+            for n, grouped in zip(sets, tiles):
+                base = 64 + A_PITCH * n
+                nc.vector.quantize_mx(
+                    out=c0_a[:, base : base + A_COLS].bitcast(FP8X4),
+                    scales=s0_a[:, base : base + A_COLS],
+                    in_=grouped[:],
                 )
-            base = 64 + A_PITCH * n
-            nc.vector.quantize_mx(
-                out=c0_a[:, base : base + A_COLS].bitcast(FP8X4),
-                scales=s0_a[:, base : base + A_COLS],
-                in_=grouped[:],
-            )
+            n0 = sets[0]
+            k = len(sets)
+            base = 64 + A_PITCH * n0
             spread(
-                lambda d: c0_a_i[:, base + 4 * d : base + 4 * d + A_COLS],
-                lambda d: s0_a_i[:, base // 4 + d : base // 4 + d + A_COLS // 4],
-                dict((s, cs_a[s][:].bitcast(I32)[:, A_COLS * n : A_COLS * (n + 1)]) for s in (0, 1, 3)),
+                lambda d: c0_a_i[:, base + 4 * d : base + 4 * d + k * A_PITCH].rearrange(
+                    "p (n c) -> p n c", c=A_PITCH
+                )[:, :, 0:A_COLS],
+                lambda d: s0_a_i[:, base // 4 + d : base // 4 + d + k * A_PITCH // 4].rearrange(
+                    "p (n c) -> p n c", c=A_PITCH // 4
+                )[:, :, 0 : A_COLS // 4],
                 dict(
-                    (s, ss_a[s][:].bitcast(I32)[:, A_COLS // 4 * n : A_COLS // 4 * (n + 1)])
-                    for s in (0, 1, 3)
+                    (
+                        s,
+                        cs_a[s][:].bitcast(I32)[:, A_COLS * n0 : A_COLS * (n0 + k)].rearrange(
+                            "p (n c) -> p n c", c=A_COLS
+                        ),
+                    )
+                    for s in MOVED
+                ),
+                dict(
+                    (
+                        s,
+                        ss_a[s][:].bitcast(I32)[:, A_COLS // 4 * n0 : A_COLS // 4 * (n0 + k)].rearrange(
+                            "p (n c) -> p n c", c=A_COLS // 4
+                        ),
+                    )
+                    for s in MOVED
                 ),
             )
 
         def prep_q():
             xw = xq[:].bitcast(F32)
+            tiles = []
             for pair in range(NSET // 2):
                 grouped = gpool.tile([P, 2, 4 * Q_COLS], BF16, tag="gq", align_bytes=64)
-                g32 = grouped[:].bitcast(F32)
+                tiles.append(grouped)
                 tp = tp_ps.tile([P, 2, 2, P], F32, tag="tp")
                 for bb in range(2):
                     for u in range(2):
                         nc.tensor.transpose(
                             tp[:, bb, u, :],
                             xw[:, 2 * pair + bb, :].rearrange("p (m u) -> p u m", u=2)[:, u, :],
-                            ident[:],
+                            perm[:],
                         )
-                for bb in range(2):
-                    nc.vector.tensor_copy(
-                        out=g32[:, bb, :].rearrange("p (w b u) -> p w b u", b=4, u=2),
-                        in_=tp[:, bb, :, :].rearrange("p u (b w) -> p w b u", b=4),
-                    )
+                nc.vector.tensor_copy(
+                    out=grouped[:].bitcast(F32).rearrange("p n (c u) -> p n c u", u=2),
+                    in_=tp[:].rearrange("p n u c -> p n c u"),
+                )
+            for pair in range(NSET // 2):
                 for bb in range(2):
                     base = 64 + Q_PITCH * (2 * pair + bb)
                     nc.vector.quantize_mx(
                         out=c0_q[:, base : base + Q_COLS].bitcast(FP8X4),
                         scales=s0_q[:, base : base + Q_COLS],
-                        in_=grouped[:, bb, :],
+                        in_=tiles[pair][:, bb, :],
                     )
             spread(
                 lambda d: c0_q_i[:, 64 + 4 * d : 64 + 4 * d + NSET * Q_PITCH].rearrange(
@@ -179,37 +222,46 @@ def tile_qa_cnn_t_kernel(tc, question, answer, W, b, out_0, out_1):
                 )[:, :, 0 : Q_COLS // 4],
                 dict(
                     (s, cs_q[s][:].bitcast(I32).rearrange("p (n c) -> p n c", c=Q_COLS))
-                    for s in (0, 1, 3)
+                    for s in MOVED
                 ),
                 dict(
                     (s, ss_q[s][:].bitcast(I32).rearrange("p (n c) -> p n c", c=Q_COLS // 4))
-                    for s in (0, 1, 3)
+                    for s in MOVED
                 ),
             )
 
+        banks = [0]
+
         def bank(h, plain_c, plain_s, plain_at, moved_c, moved_s, moved_at, dest):
             acc = mm_ps.tile([P, 4, P], F32, tag="mm")
-            for s in (2, 1, 0, 3):
-                if s == 2:
-                    codes, planes, at = plain_c, plain_s, plain_at
-                else:
-                    codes, planes, at = moved_c[s], moved_s[s], moved_at
+            cols = slice(P * h, P * h + P)
+
+            def one(s, weights, codes, planes, at, start, stop):
                 nc.tensor.matmul_mx(
                     out=acc[:, s, :],
-                    lhsT=wq[:, s, P * h : P * h + P].bitcast(FP8X4),
-                    lhsT_scale=wqs[:, s, P * h : P * h + P],
+                    lhsT=weights.bitcast(FP8X4),
+                    lhsT_scale=wqs[:, s, cols],
                     rhs=codes[:, at : at + P].bitcast(FP8X4),
                     rhs_scale=planes[:, at : at + P],
-                    start=True,
-                    stop=True,
+                    start=start,
+                    stop=stop,
                 )
-            nc.scalar.activation(
-                out=dest.rearrange("c b (u s) -> c u b s", s=4),
-                in_=acc[:].rearrange("c s (u b) -> c u b s", b=4),
-                func=IDENTITY,
-                bias=bias[:, h : h + 1],
-                scale=1.0,
-            )
+
+            one(2, wq[:, 2, cols], plain_c, plain_s, plain_at, True, True)
+            one(1, wq[:, 1, cols], moved_c[1], moved_s[1], moved_at, True, True)
+            one(0, wq[:, 0, cols], moved_c[0], moved_s[0], moved_at, True, True)
+            one(3, wq[:, 3, cols], moved_c[3], moved_s[3], moved_at, True, True)
+            banks[0] += 1
+            o_view = dest.rearrange("c b (u s) -> c u b s", s=4)
+            a_view = acc[:].rearrange("c s (u b) -> c u b s", b=4)
+            if banks[0] % VEC_EVERY == 0:
+                nc.vector.tensor_scalar(
+                    out=o_view, in0=a_view, scalar1=bias[:, h : h + 1], scalar2=None, op0=ADD
+                )
+            else:
+                nc.scalar.activation(
+                    out=o_view, in_=a_view, func=IDENTITY, bias=bias[:, h : h + 1], scale=1.0
+                )
 
         def run_a(n):
             for h in range(2):
@@ -240,13 +292,18 @@ def tile_qa_cnn_t_kernel(tc, question, answer, W, b, out_0, out_1):
                     in_=o[:],
                 )
 
-        prep_a(0)
-        prep_a(1)
-        for n in range(NSET):
-            run_a(n)
-            if n + 2 < NSET:
-                prep_a(n + 2)
-            if n == NSET - 2:
-                prep_q()
+        prep_a([0], prep_w)
+        for s in (2, 0, 3, 1):
+            quant_w(s)
+        prep_a([1])
+        run_a(0)
+        prep_a([2, 3])
+        run_a(1)
+        run_a(2)
+        prep_a([4, 5])
+        run_a(3)
+        prep_q()
+        run_a(4)
+        run_a(5)
         for pair in range(NSET // 2):
             run_q(pair)

@@ -13,6 +13,7 @@ U8 = mybir.dt.uint8
 FP8X4 = mybir.dt.float8_e4m3fn_x4
 IDENTITY = mybir.ActivationFunctionType.Identity
 ADD = mybir.AluOpType.add
+MULT = mybir.AluOpType.mult
 
 P = 128
 NSET = 6
@@ -20,8 +21,9 @@ A_COLS = 512
 A_PITCH = 576
 Q_COLS = 128
 Q_PITCH = 192
-MOVED = (0, 1, 3)
-VEC_EVERY = 5
+MOVED = (0, 3)
+VEC_A = {0: (3,), 1: (3,), 2: (3,), 3: (3,), 4: (3,), 5: (1, 3, 5, 7)}
+VEC_Q = (1, 3)
 
 
 def tile_qa_cnn_t_kernel(tc, question, answer, W, b, out_0, out_1):
@@ -32,20 +34,27 @@ def tile_qa_cnn_t_kernel(tc, question, answer, W, b, out_0, out_1):
         opool = ctx.enter_context(tc.tile_pool(name="outs", bufs=4))
         tp_ps = ctx.enter_context(tc.psum_pool(name="tp", bufs=2))
         mm_ps = ctx.enter_context(tc.psum_pool(name="mm", bufs=6))
+        ctx.enter_context(tc.manual_schedule())
 
-        w_raw = keep.tile([P, 1024], BF16, name="w_raw")
-        nc.sync.dma_start(out=w_raw[:], in_=W.rearrange("(p t) c -> p (t c)", t=4))
-        b_bf = keep.tile([P, 2], BF16, name="b_bf")
-        with nc.allow_non_contiguous_dma(reason="256 bias values, one to a partition"):
-            nc.scalar.dma_start(out=b_bf[:], in_=b.rearrange("(h c) -> c h", h=2))
         a_rows = answer.flatten_outer_dims().rearrange(
             "(n b w g) e -> n w b (g e)", n=NSET, b=4, g=4
         )
+        w_rows = W.rearrange("(p t) c -> p (t c)", t=4)
         xa = []
         for n in range(NSET):
-            x = keep.tile([P, 4, 512], BF16, name="xa%d" % n)
-            nc.sync.dma_start(out=x[:], in_=a_rows[n])
-            xa.append(x)
+            xa.append(keep.tile([P, 4, 512], BF16, name="xa%d" % n))
+        w_raw = keep.tile([P, 4, 1024], BF16, name="w_raw")
+        nc.sync.dma_start(out=xa[0][:], in_=a_rows[0])
+        nc.sync.dma_start(out=w_raw[:, 2, :], in_=w_rows)
+        for s in (0, 3, 1):
+            rot = 32 * ((2 - s) % 4)
+            nc.scalar.dma_start(out=w_raw[0 : P - rot, s, :], in_=w_rows[rot:P, :])
+            nc.scalar.dma_start(out=w_raw[P - rot : P, s, :], in_=w_rows[0:rot, :])
+        b_bf = keep.tile([P, 2], BF16, name="b_bf")
+        with nc.allow_non_contiguous_dma(reason="256 bias values, one to a partition"):
+            nc.scalar.dma_start(out=b_bf[:], in_=b.rearrange("(h c) -> c h", h=2))
+        for n in range(1, NSET):
+            nc.sync.dma_start(out=xa[n][:], in_=a_rows[n])
         xq = keep.tile([P, NSET, 512], BF16, name="xq")
         nc.sync.dma_start(
             out=xq[:],
@@ -54,18 +63,6 @@ def tile_qa_cnn_t_kernel(tc, question, answer, W, b, out_0, out_1):
 
         ident = keep.tile([P, P], F32, name="ident")
         make_identity(nc, ident[:])
-        ident_b = keep.tile([P, P], BF16, name="ident_b")
-        make_identity(nc, ident_b[:])
-        twice = keep.tile([P, 2 * P], BF16, name="twice")
-        nc.vector.tensor_copy(out=twice[:, 0:P], in_=ident_b[:])
-        nc.vector.tensor_copy(out=twice[:, P : 2 * P], in_=ident_b[:])
-        perm = keep.tile([P, P], F32, name="perm")
-        nc.vector.tensor_copy(
-            out=perm[:].rearrange("p (w b) -> p w b", b=4),
-            in_=ident[:].rearrange("p (b w) -> p w b", b=4),
-        )
-        bias = keep.tile([P, 2], F32, name="bias")
-        nc.vector.tensor_copy(out=bias[:], in_=b_bf[:])
 
         c0_a = keep.tile([P, 7 * A_PITCH], U32, name="c0_a", align_bytes=64)
         s0_a = keep.tile([P, 7 * A_PITCH], U8, name="s0_a", align_bytes=64)
@@ -89,35 +86,44 @@ def tile_qa_cnn_t_kernel(tc, question, answer, W, b, out_0, out_1):
             cs_q[s] = keep.tile([P, NSET * Q_COLS], U32, name="cs_q%d" % s, align_bytes=64)
             ss_q[s] = keep.tile([P, NSET * Q_COLS], U8, name="ss_q%d" % s, align_bytes=64)
 
-        w_view = w_raw[:].rearrange("p (t c) -> p t c", t=4)
-        w_grp = keep.tile([P, 4, 2, P, 4], BF16, name="w_grp", align_bytes=64)
+        w_grp = keep.tile([P, 4, 256, 4], BF16, name="w_grp", align_bytes=64)
         wq = keep.tile([P, 4, 256], U32, name="wq", align_bytes=64)
         wqs = keep.tile([P, 4, 256], U8, name="wqs", align_bytes=64)
+        w1a = keep.tile([P, 256], U32, name="w1a", align_bytes=64)
+        w1b = keep.tile([P, 256], U32, name="w1b", align_bytes=64)
+        nc.vector.memset(w1a[:].bitcast(I32), 0)
+        nc.vector.memset(w1b[:].bitcast(I32), 0)
+        perm = keep.tile([P, P], F32, name="perm")
+        nc.vector.tensor_copy(
+            out=perm[:].rearrange("p (w b) -> p w b", b=4),
+            in_=ident[:].rearrange("p (b w) -> p w b", b=4),
+        )
+        bias = keep.tile([P, 2], F32, name="bias")
 
-        def prep_w():
-            nc.scalar.copy(
-                out=w_grp[:, 2].rearrange("p h c t -> p (h c) t"),
-                in_=w_view.rearrange("p t c -> p c t"),
-            )
-            for s in (0, 3, 1):
-                rot = (2 - s) % 4
-                for h in range(2):
-                    ps = mm_ps.tile([P, 4, P], F32, tag="mm")
-                    nc.tensor.matmul(
-                        out=ps[:],
-                        lhsT=twice[:, 32 * rot : 32 * rot + P],
-                        rhs=w_view[:, :, P * h : P * h + P],
-                        start=True,
-                        stop=True,
-                    )
-                    nc.scalar.copy(out=w_grp[:, s, h], in_=ps[:].rearrange("p t c -> p c t"))
+        def regroup_w():
+            for s in (2, 0):
+                nc.scalar.copy(out=w_grp[:, s], in_=w_raw[:, s, :].rearrange("p (t c) -> p c t", t=4))
+            for s in (3, 1):
+                nc.gpsimd.tensor_scalar(
+                    out=w_grp[:, s],
+                    in0=w_raw[:, s, :].rearrange("p (t c) -> p c t", t=4),
+                    scalar1=1.0,
+                    scalar2=0.0,
+                    op0=MULT,
+                    op1=ADD,
+                )
 
         def quant_w(s):
             nc.vector.quantize_mx(
                 out=wq[:, s, :].bitcast(FP8X4),
                 scales=wqs[:, s, :],
-                in_=w_grp[:, s].rearrange("p h c t -> p (h c t)"),
+                in_=w_grp[:, s].rearrange("p c t -> p (c t)"),
             )
+            if s == 1:
+                nc.vector.tensor_copy(out=w1a[:].bitcast(I32)[0:96], in_=wq[:, 1, :].bitcast(I32)[0:96])
+                nc.vector.tensor_copy(
+                    out=w1b[:].bitcast(I32)[96:128], in_=wq[:, 1, :].bitcast(I32)[96:128]
+                )
 
         def spread(src_c, src_s, dst_c, dst_s):
             for src, dst in ((src_c, dst_c), (src_s, dst_s)):
@@ -125,67 +131,55 @@ def tile_qa_cnn_t_kernel(tc, question, answer, W, b, out_0, out_1):
                 nc.vector.tensor_copy(out=dst[0][0:64], in_=src(0)[0:64])
                 nc.vector.tensor_copy(out=dst[0][64:128], in_=src(-1)[64:128])
                 nc.vector.tensor_copy(out=dst[3][0:32], in_=src(1)[0:32])
-                nc.vector.tensor_copy(out=dst[1][0:96], in_=src(0)[0:96])
-                nc.vector.tensor_copy(out=dst[1][96:128], in_=src(-1)[96:128])
 
-        def prep_a(sets, between=None):
-            tiles = []
-            for n in sets:
-                xw = xa[n][:].bitcast(F32)
-                grouped = gpool.tile([P, 4 * A_COLS], BF16, tag="ga", align_bytes=64)
-                tiles.append(grouped)
-                g32 = grouped[:].bitcast(F32).rearrange("p (w b u) -> p w b u", b=4, u=2)
-                for half in range(2):
-                    tp = tp_ps.tile([P, 2, 2, P], F32, tag="tp")
-                    for bb in range(2):
-                        for u in range(2):
-                            nc.tensor.transpose(
-                                tp[:, bb, u, :],
-                                xw[:, 2 * half + bb, :].rearrange("p (m u) -> p u m", u=2)[:, u, :],
-                                ident[:],
-                            )
-                    nc.vector.tensor_copy(
-                        out=g32[:, :, 2 * half : 2 * half + 2, :],
-                        in_=tp[:].rearrange("p b u w -> p w b u"),
-                    )
-            if between is not None:
-                between()
-            for n, grouped in zip(sets, tiles):
-                base = 64 + A_PITCH * n
-                nc.vector.quantize_mx(
-                    out=c0_a[:, base : base + A_COLS].bitcast(FP8X4),
-                    scales=s0_a[:, base : base + A_COLS],
-                    in_=grouped[:],
+        def turn_a(n):
+            xw = xa[n][:].bitcast(F32)
+            turned = []
+            for half in range(2):
+                tp = tp_ps.tile([P, 2, 2, P], F32, tag="tp")
+                turned.append(tp)
+                for bb in range(2):
+                    for u in range(2):
+                        nc.tensor.transpose(
+                            tp[:, bb, u, :],
+                            xw[:, 2 * half + bb, :].rearrange("p (m u) -> p u m", u=2)[:, u, :],
+                            ident[:],
+                        )
+            return turned
+
+        def group_a(turned):
+            grouped = gpool.tile([P, 4 * A_COLS], BF16, tag="ga", align_bytes=64)
+            g32 = grouped[:].bitcast(F32).rearrange("p (w b u) -> p w b u", b=4, u=2)
+            for half in range(2):
+                nc.vector.tensor_copy(
+                    out=g32[:, :, 2 * half : 2 * half + 2, :],
+                    in_=turned[half][:].rearrange("p b u w -> p w b u"),
                 )
-            n0 = sets[0]
-            k = len(sets)
-            base = 64 + A_PITCH * n0
+            return grouped
+
+        def quant_a(n, grouped):
+            base = 64 + A_PITCH * n
+            nc.vector.quantize_mx(
+                out=c0_a[:, base : base + A_COLS].bitcast(FP8X4),
+                scales=s0_a[:, base : base + A_COLS],
+                in_=grouped[:],
+            )
+
+        def spread_a(n):
+            base = 64 + A_PITCH * n
             spread(
-                lambda d: c0_a_i[:, base + 4 * d : base + 4 * d + k * A_PITCH].rearrange(
-                    "p (n c) -> p n c", c=A_PITCH
-                )[:, :, 0:A_COLS],
-                lambda d: s0_a_i[:, base // 4 + d : base // 4 + d + k * A_PITCH // 4].rearrange(
-                    "p (n c) -> p n c", c=A_PITCH // 4
-                )[:, :, 0 : A_COLS // 4],
+                lambda d: c0_a_i[:, base + 4 * d : base + 4 * d + A_COLS],
+                lambda d: s0_a_i[:, base // 4 + d : base // 4 + d + A_COLS // 4],
+                dict((s, cs_a[s][:].bitcast(I32)[:, A_COLS * n : A_COLS * (n + 1)]) for s in MOVED),
                 dict(
-                    (
-                        s,
-                        cs_a[s][:].bitcast(I32)[:, A_COLS * n0 : A_COLS * (n0 + k)].rearrange(
-                            "p (n c) -> p n c", c=A_COLS
-                        ),
-                    )
-                    for s in MOVED
-                ),
-                dict(
-                    (
-                        s,
-                        ss_a[s][:].bitcast(I32)[:, A_COLS // 4 * n0 : A_COLS // 4 * (n0 + k)].rearrange(
-                            "p (n c) -> p n c", c=A_COLS // 4
-                        ),
-                    )
+                    (s, ss_a[s][:].bitcast(I32)[:, A_COLS // 4 * n : A_COLS // 4 * (n + 1)])
                     for s in MOVED
                 ),
             )
+
+        def prep_a(n):
+            quant_a(n, group_a(turn_a(n)))
+            spread_a(n)
 
         def prep_q():
             xw = xq[:].bitcast(F32)
@@ -230,9 +224,7 @@ def tile_qa_cnn_t_kernel(tc, question, answer, W, b, out_0, out_1):
                 ),
             )
 
-        banks = [0]
-
-        def bank(h, plain_c, plain_s, plain_at, moved_c, moved_s, moved_at, dest):
+        def bank(h, on_vector, plain_c, plain_s, plain_at, moved_c, moved_s, moved_at, dest):
             acc = mm_ps.tile([P, 4, P], F32, tag="mm")
             cols = slice(P * h, P * h + P)
 
@@ -248,13 +240,13 @@ def tile_qa_cnn_t_kernel(tc, question, answer, W, b, out_0, out_1):
                 )
 
             one(2, wq[:, 2, cols], plain_c, plain_s, plain_at, True, True)
-            one(1, wq[:, 1, cols], moved_c[1], moved_s[1], moved_at, True, True)
+            one(1, w1a[:, cols], plain_c, plain_s, plain_at, True, False)
+            one(1, w1b[:, cols], moved_c[0], moved_s[0], moved_at, False, True)
             one(0, wq[:, 0, cols], moved_c[0], moved_s[0], moved_at, True, True)
             one(3, wq[:, 3, cols], moved_c[3], moved_s[3], moved_at, True, True)
-            banks[0] += 1
             o_view = dest.rearrange("c b (u s) -> c u b s", s=4)
             a_view = acc[:].rearrange("c s (u b) -> c u b s", b=4)
-            if banks[0] % VEC_EVERY == 0:
+            if on_vector:
                 nc.vector.tensor_scalar(
                     out=o_view, in0=a_view, scalar1=bias[:, h : h + 1], scalar2=None, op0=ADD
                 )
@@ -263,12 +255,13 @@ def tile_qa_cnn_t_kernel(tc, question, answer, W, b, out_0, out_1):
                     out=o_view, in_=a_view, func=IDENTITY, bias=bias[:, h : h + 1], scale=1.0
                 )
 
-        def run_a(n):
+        def run_a(n, mid=None):
             for h in range(2):
                 o = opool.tile([P, 4, 512], F32, tag="oa")
                 for v in range(4):
                     bank(
-                        h, c0_a, s0_a, 64 + A_PITCH * n + P * v,
+                        h, (4 * h + v) in VEC_A[n],
+                        c0_a, s0_a, 64 + A_PITCH * n + P * v,
                         cs_a, ss_a, A_COLS * n + P * v,
                         o[:, :, P * v : P * v + P],
                     )
@@ -276,6 +269,8 @@ def tile_qa_cnn_t_kernel(tc, question, answer, W, b, out_0, out_1):
                     out=out_1[4 * n : 4 * n + 4, P * h : P * h + P, :].rearrange("b c i -> c b i"),
                     in_=o[:],
                 )
+                if h == 0 and mid is not None:
+                    mid()
 
         def run_q(pair):
             for h in range(2):
@@ -283,7 +278,8 @@ def tile_qa_cnn_t_kernel(tc, question, answer, W, b, out_0, out_1):
                 for bb in range(2):
                     n = 2 * pair + bb
                     bank(
-                        h, c0_q, s0_q, 64 + Q_PITCH * n,
+                        h, (2 * h + bb) in VEC_Q,
+                        c0_q, s0_q, 64 + Q_PITCH * n,
                         cs_q, ss_q, Q_COLS * n,
                         o[:, 4 * bb : 4 * bb + 4, :],
                     )
@@ -292,18 +288,23 @@ def tile_qa_cnn_t_kernel(tc, question, answer, W, b, out_0, out_1):
                     in_=o[:],
                 )
 
-        prep_a([0], prep_w)
-        for s in (2, 0, 3, 1):
-            quant_w(s)
-        prep_a([1])
-        run_a(0)
-        prep_a([2, 3])
-        run_a(1)
-        run_a(2)
-        prep_a([4, 5])
-        run_a(3)
-        prep_q()
-        run_a(4)
+        g0 = group_a(turn_a(0))
+        regroup_w()
+        quant_a(0, g0)
+        quant_w(2)
+        quant_w(0)
+        t1 = turn_a(1)
+        spread_a(0)
+        quant_w(3)
+        quant_w(1)
+        nc.vector.tensor_copy(out=bias[:], in_=b_bf[:])
+        quant_a(1, group_a(t1))
+        spread_a(1)
+        run_a(0, lambda: prep_a(2))
+        run_a(1, lambda: prep_a(3))
+        run_a(2, lambda: prep_a(4))
+        run_a(3, lambda: prep_a(5))
+        run_a(4, prep_q)
         run_a(5)
         for pair in range(NSET // 2):
             run_q(pair)

@@ -31,20 +31,18 @@ def tile_qa_cnn_t_kernel(tc, question, answer, W, b, out_0, out_1):
     with ExitStack() as ctx:
         keep = ctx.enter_context(tc.tile_pool(name="keep", bufs=1))
         gpool = ctx.enter_context(tc.tile_pool(name="grouped", bufs=3))
-        opool = ctx.enter_context(tc.tile_pool(name="outs", bufs=4))
+        opool = ctx.enter_context(tc.tile_pool(name="outs", bufs=3))
         tp_ps = ctx.enter_context(tc.psum_pool(name="tp", bufs=2))
         mm_ps = ctx.enter_context(tc.psum_pool(name="mm", bufs=6))
         ctx.enter_context(tc.manual_schedule())
 
-        a_rows = answer.flatten_outer_dims().rearrange(
-            "(n b w g) e -> n w b (g e)", n=NSET, b=4, g=4
-        )
+        a_rows = answer.flatten_outer_dims().rearrange("(n k f) e -> n k (f e)", n=NSET, f=16)
         w_rows = W.rearrange("(p t) c -> p (t c)", t=4)
         xa = []
         for n in range(NSET):
             xa.append(keep.tile([P, 4, 512], BF16, name="xa%d" % n))
         w_raw = keep.tile([P, 4, 1024], BF16, name="w_raw")
-        nc.sync.dma_start(out=xa[0][:], in_=a_rows[0])
+        nc.sync.dma_start(out=xa[0][:].rearrange("p l f -> p (l f)"), in_=a_rows[0])
         nc.sync.dma_start(out=w_raw[:, 2, :], in_=w_rows)
         for s in (0, 3, 1):
             rot = 32 * ((2 - s) % 4)
@@ -52,9 +50,9 @@ def tile_qa_cnn_t_kernel(tc, question, answer, W, b, out_0, out_1):
             nc.scalar.dma_start(out=w_raw[P - rot : P, s, :], in_=w_rows[0:rot, :])
         b_bf = keep.tile([P, 2], BF16, name="b_bf")
         with nc.allow_non_contiguous_dma(reason="256 bias values, one to a partition"):
-            nc.scalar.dma_start(out=b_bf[:], in_=b.rearrange("(h c) -> c h", h=2))
+            nc.scalar.dma_start(out=b_bf[:], in_=b.rearrange("(c h) -> c h", h=2))
         for n in range(1, NSET):
-            nc.sync.dma_start(out=xa[n][:], in_=a_rows[n])
+            nc.sync.dma_start(out=xa[n][:].rearrange("p l f -> p (l f)"), in_=a_rows[n])
         xq = keep.tile([P, NSET, 512], BF16, name="xq")
         nc.sync.dma_start(
             out=xq[:],
@@ -102,11 +100,14 @@ def tile_qa_cnn_t_kernel(tc, question, answer, W, b, out_0, out_1):
 
         def regroup_w():
             for s in (2, 0):
-                nc.scalar.copy(out=w_grp[:, s], in_=w_raw[:, s, :].rearrange("p (t c) -> p c t", t=4))
+                nc.scalar.copy(
+                    out=w_grp[:, s].rearrange("p (h m) t -> p h m t", h=2),
+                    in_=w_raw[:, s, :].rearrange("p (t m h) -> p h m t", t=4, h=2),
+                )
             for s in (3, 1):
                 nc.gpsimd.tensor_scalar(
-                    out=w_grp[:, s],
-                    in0=w_raw[:, s, :].rearrange("p (t c) -> p c t", t=4),
+                    out=w_grp[:, s].rearrange("p (h m) t -> p h m t", h=2),
+                    in0=w_raw[:, s, :].rearrange("p (t m h) -> p h m t", t=4, h=2),
                     scalar1=1.0,
                     scalar2=0.0,
                     op0=MULT,
@@ -143,17 +144,17 @@ def tile_qa_cnn_t_kernel(tc, question, answer, W, b, out_0, out_1):
                         nc.tensor.transpose(
                             tp[:, bb, u, :],
                             xw[:, 2 * half + bb, :].rearrange("p (m u) -> p u m", u=2)[:, u, :],
-                            ident[:],
+                            perm[:],
                         )
             return turned
 
         def group_a(turned):
             grouped = gpool.tile([P, 4 * A_COLS], BF16, tag="ga", align_bytes=64)
-            g32 = grouped[:].bitcast(F32).rearrange("p (w b u) -> p w b u", b=4, u=2)
+            g32 = grouped[:].bitcast(F32).rearrange("p (w l b u) -> p w l b u", l=4, b=4, u=2)
             for half in range(2):
                 nc.vector.tensor_copy(
-                    out=g32[:, :, 2 * half : 2 * half + 2, :],
-                    in_=turned[half][:].rearrange("p b u w -> p w b u"),
+                    out=g32[:, :, 2 * half : 2 * half + 2, :, :],
+                    in_=turned[half][:].rearrange("p l u (w b) -> p w l b u", b=4),
                 )
             return grouped
 
@@ -256,37 +257,45 @@ def tile_qa_cnn_t_kernel(tc, question, answer, W, b, out_0, out_1):
                 )
 
         def run_a(n, mid=None):
+            o = opool.tile([P, 4, 2, 512], F32, tag="oa")
+            rows = out_1[4 * n : 4 * n + 4].rearrange("b (m h) i -> m b h i", h=2)
             for h in range(2):
-                o = opool.tile([P, 4, 512], F32, tag="oa")
                 for v in range(4):
                     bank(
                         h, (4 * h + v) in VEC_A[n],
                         c0_a, s0_a, 64 + A_PITCH * n + P * v,
                         cs_a, ss_a, A_COLS * n + P * v,
-                        o[:, :, P * v : P * v + P],
+                        o[:, :, h, P * v : P * v + P],
                     )
-                nc.sync.dma_start(
-                    out=out_1[4 * n : 4 * n + 4, P * h : P * h + P, :].rearrange("b c i -> c b i"),
-                    in_=o[:],
-                )
+                if n == 0:
+                    nc.sync.dma_start(out=rows[:, :, h, :], in_=o[:, :, h, :])
+                elif h == 1:
+                    nc.sync.dma_start(
+                        out=rows.rearrange("m b h i -> m b (h i)"),
+                        in_=o[:].rearrange("m b h i -> m b (h i)"),
+                    )
                 if h == 0 and mid is not None:
                     mid()
 
         def run_q(pair):
-            for h in range(2):
-                o = opool.tile([P, 8, P], F32, tag="oq")
-                for bb in range(2):
-                    n = 2 * pair + bb
+            o = opool.tile([P, 8, 2, P], F32, tag="oq")
+            rows = out_0[8 * pair : 8 * pair + 8].rearrange("b (m h) i -> m b (h i)", h=2)
+            flat = o[:].rearrange("m b h i -> m b (h i)")
+            for bb in range(2):
+                n = 2 * pair + bb
+                for h in range(2):
                     bank(
-                        h, (2 * h + bb) in VEC_Q,
+                        h, (2 * bb + h) in VEC_Q,
                         c0_q, s0_q, 64 + Q_PITCH * n,
                         cs_q, ss_q, Q_COLS * n,
-                        o[:, 4 * bb : 4 * bb + 4, :],
+                        o[:, 4 * bb : 4 * bb + 4, h, :],
                     )
-                nc.sync.dma_start(
-                    out=out_0[8 * pair : 8 * pair + 8, P * h : P * h + P, :].rearrange("b c i -> c b i"),
-                    in_=o[:],
-                )
+                if pair == NSET // 2 - 1:
+                    nc.sync.dma_start(
+                        out=rows[:, 4 * bb : 4 * bb + 4, :], in_=flat[:, 4 * bb : 4 * bb + 4, :]
+                    )
+            if pair < NSET // 2 - 1:
+                nc.sync.dma_start(out=rows, in_=flat)
 
         g0 = group_a(turn_a(0))
         regroup_w()

@@ -31,18 +31,20 @@ def tile_qa_cnn_t_kernel(tc, question, answer, W, b, out_0, out_1):
     with ExitStack() as ctx:
         keep = ctx.enter_context(tc.tile_pool(name="keep", bufs=1))
         gpool = ctx.enter_context(tc.tile_pool(name="grouped", bufs=3))
-        opool = ctx.enter_context(tc.tile_pool(name="outs", bufs=3))
+        opool = ctx.enter_context(tc.tile_pool(name="outs", bufs=4))
         tp_ps = ctx.enter_context(tc.psum_pool(name="tp", bufs=2))
         mm_ps = ctx.enter_context(tc.psum_pool(name="mm", bufs=6))
         ctx.enter_context(tc.manual_schedule())
 
-        a_rows = answer.flatten_outer_dims().rearrange("(n k f) e -> n k (f e)", n=NSET, f=16)
+        a_rows = answer.flatten_outer_dims().rearrange(
+            "(n b w g) e -> n w b (g e)", n=NSET, b=4, g=4
+        )
         w_rows = W.rearrange("(p t) c -> p (t c)", t=4)
         xa = []
         for n in range(NSET):
             xa.append(keep.tile([P, 4, 512], BF16, name="xa%d" % n))
         w_raw = keep.tile([P, 4, 1024], BF16, name="w_raw")
-        nc.sync.dma_start(out=xa[0][:].rearrange("p l f -> p (l f)"), in_=a_rows[0])
+        nc.sync.dma_start(out=xa[0][:], in_=a_rows[0])
         nc.sync.dma_start(out=w_raw[:, 2, :], in_=w_rows)
         for s in (0, 3, 1):
             rot = 32 * ((2 - s) % 4)
@@ -50,9 +52,9 @@ def tile_qa_cnn_t_kernel(tc, question, answer, W, b, out_0, out_1):
             nc.scalar.dma_start(out=w_raw[P - rot : P, s, :], in_=w_rows[0:rot, :])
         b_bf = keep.tile([P, 2], BF16, name="b_bf")
         with nc.allow_non_contiguous_dma(reason="256 bias values, one to a partition"):
-            nc.scalar.dma_start(out=b_bf[:], in_=b.rearrange("(c h) -> c h", h=2))
+            nc.scalar.dma_start(out=b_bf[:], in_=b.rearrange("(h c) -> c h", h=2))
         for n in range(1, NSET):
-            nc.sync.dma_start(out=xa[n][:].rearrange("p l f -> p (l f)"), in_=a_rows[n])
+            nc.sync.dma_start(out=xa[n][:], in_=a_rows[n])
         xq = keep.tile([P, NSET, 512], BF16, name="xq")
         nc.sync.dma_start(
             out=xq[:],
@@ -100,14 +102,11 @@ def tile_qa_cnn_t_kernel(tc, question, answer, W, b, out_0, out_1):
 
         def regroup_w():
             for s in (2, 0):
-                nc.scalar.copy(
-                    out=w_grp[:, s].rearrange("p (h m) t -> p h m t", h=2),
-                    in_=w_raw[:, s, :].rearrange("p (t m h) -> p h m t", t=4, h=2),
-                )
+                nc.scalar.copy(out=w_grp[:, s], in_=w_raw[:, s, :].rearrange("p (t c) -> p c t", t=4))
             for s in (3, 1):
                 nc.gpsimd.tensor_scalar(
-                    out=w_grp[:, s].rearrange("p (h m) t -> p h m t", h=2),
-                    in0=w_raw[:, s, :].rearrange("p (t m h) -> p h m t", t=4, h=2),
+                    out=w_grp[:, s],
+                    in0=w_raw[:, s, :].rearrange("p (t c) -> p c t", t=4),
                     scalar1=1.0,
                     scalar2=0.0,
                     op0=MULT,
@@ -144,17 +143,17 @@ def tile_qa_cnn_t_kernel(tc, question, answer, W, b, out_0, out_1):
                         nc.tensor.transpose(
                             tp[:, bb, u, :],
                             xw[:, 2 * half + bb, :].rearrange("p (m u) -> p u m", u=2)[:, u, :],
-                            perm[:],
+                            ident[:],
                         )
             return turned
 
         def group_a(turned):
             grouped = gpool.tile([P, 4 * A_COLS], BF16, tag="ga", align_bytes=64)
-            g32 = grouped[:].bitcast(F32).rearrange("p (w l b u) -> p w l b u", l=4, b=4, u=2)
+            g32 = grouped[:].bitcast(F32).rearrange("p (w b u) -> p w b u", b=4, u=2)
             for half in range(2):
                 nc.vector.tensor_copy(
-                    out=g32[:, :, 2 * half : 2 * half + 2, :, :],
-                    in_=turned[half][:].rearrange("p l u (w b) -> p w l b u", b=4),
+                    out=g32[:, :, 2 * half : 2 * half + 2, :],
+                    in_=turned[half][:].rearrange("p b u w -> p w b u"),
                 )
             return grouped
 
@@ -245,8 +244,8 @@ def tile_qa_cnn_t_kernel(tc, question, answer, W, b, out_0, out_1):
             one(1, w1b[:, cols], moved_c[0], moved_s[0], moved_at, False, True)
             one(0, wq[:, 0, cols], moved_c[0], moved_s[0], moved_at, True, True)
             one(3, wq[:, 3, cols], moved_c[3], moved_s[3], moved_at, True, True)
-            o_view = dest.rearrange("c b (u s) -> c u b s", s=4)
-            a_view = acc[:].rearrange("c s (u b) -> c u b s", b=4)
+            o_view = dest.rearrange("c b (u s) -> c u s b", s=4)
+            a_view = acc[:].rearrange("c s (u b) -> c u s b", b=4)
             if on_vector:
                 nc.vector.tensor_scalar(
                     out=o_view, in0=a_view, scalar1=bias[:, h : h + 1], scalar2=None, op0=ADD
@@ -257,45 +256,37 @@ def tile_qa_cnn_t_kernel(tc, question, answer, W, b, out_0, out_1):
                 )
 
         def run_a(n, mid=None):
-            o = opool.tile([P, 4, 2, 512], F32, tag="oa")
-            rows = out_1[4 * n : 4 * n + 4].rearrange("b (m h) i -> m b h i", h=2)
             for h in range(2):
+                o = opool.tile([P, 4, 512], F32, tag="oa")
                 for v in range(4):
                     bank(
                         h, (4 * h + v) in VEC_A[n],
                         c0_a, s0_a, 64 + A_PITCH * n + P * v,
                         cs_a, ss_a, A_COLS * n + P * v,
-                        o[:, :, h, P * v : P * v + P],
+                        o[:, :, P * v : P * v + P],
                     )
-                if n == 0:
-                    nc.sync.dma_start(out=rows[:, :, h, :], in_=o[:, :, h, :])
-                elif h == 1:
-                    nc.sync.dma_start(
-                        out=rows.rearrange("m b h i -> m b (h i)"),
-                        in_=o[:].rearrange("m b h i -> m b (h i)"),
-                    )
+                nc.sync.dma_start(
+                    out=out_1[4 * n : 4 * n + 4, P * h : P * h + P, :].rearrange("b c i -> c b i"),
+                    in_=o[:],
+                )
                 if h == 0 and mid is not None:
                     mid()
 
         def run_q(pair):
-            o = opool.tile([P, 8, 2, P], F32, tag="oq")
-            rows = out_0[8 * pair : 8 * pair + 8].rearrange("b (m h) i -> m b (h i)", h=2)
-            flat = o[:].rearrange("m b h i -> m b (h i)")
-            for bb in range(2):
-                n = 2 * pair + bb
-                for h in range(2):
+            for h in range(2):
+                o = opool.tile([P, 8, P], F32, tag="oq")
+                for bb in range(2):
+                    n = 2 * pair + bb
                     bank(
-                        h, (2 * bb + h) in VEC_Q,
+                        h, (2 * h + bb) in VEC_Q,
                         c0_q, s0_q, 64 + Q_PITCH * n,
                         cs_q, ss_q, Q_COLS * n,
-                        o[:, 4 * bb : 4 * bb + 4, h, :],
+                        o[:, 4 * bb : 4 * bb + 4, :],
                     )
-                if pair == NSET // 2 - 1:
-                    nc.sync.dma_start(
-                        out=rows[:, 4 * bb : 4 * bb + 4, :], in_=flat[:, 4 * bb : 4 * bb + 4, :]
-                    )
-            if pair < NSET // 2 - 1:
-                nc.sync.dma_start(out=rows, in_=flat)
+                nc.sync.dma_start(
+                    out=out_0[8 * pair : 8 * pair + 8, P * h : P * h + P, :].rearrange("b c i -> c b i"),
+                    in_=o[:],
+                )
 
         g0 = group_a(turn_a(0))
         regroup_w()

@@ -21,7 +21,8 @@ A_COLS = 512
 A_PITCH = 576
 Q_COLS = 128
 Q_PITCH = 192
-MOVED = (0, 3)
+PLAIN_PARTS = {0: ((0, 64),), 1: ((0, 96),), 3: ((32, 64), (64, 128))}
+SHIFTED_PARTS = {0: ((64, 128),), 1: ((96, 128),), 3: ((0, 32),)}
 VEC_A = {0: (3,), 1: (3,), 2: (3,), 3: (3,), 4: (3,), 5: (1, 3, 5, 7)}
 VEC_Q = (1, 3)
 
@@ -76,23 +77,20 @@ def tile_qa_cnn_t_kernel(tc, question, answer, W, b, out_0, out_1):
         nc.vector.memset(s0_a_i, 0)
         nc.vector.memset(c0_q_i.rearrange("p (n c) -> p n c", c=Q_PITCH)[:, :, 0:64], 0)
         nc.vector.memset(s0_q_i, 0)
-        cs_a = {}
-        ss_a = {}
-        cs_q = {}
-        ss_q = {}
-        for s in MOVED:
-            cs_a[s] = keep.tile([P, NSET * A_COLS], U32, name="cs_a%d" % s, align_bytes=64)
-            ss_a[s] = keep.tile([P, NSET * A_COLS], U8, name="ss_a%d" % s, align_bytes=64)
-            cs_q[s] = keep.tile([P, NSET * Q_COLS], U32, name="cs_q%d" % s, align_bytes=64)
-            ss_q[s] = keep.tile([P, NSET * Q_COLS], U8, name="ss_q%d" % s, align_bytes=64)
+        cs_a = keep.tile([P, NSET * A_COLS], U32, name="cs_a", align_bytes=64)
+        ss_a = keep.tile([P, NSET * A_COLS], U8, name="ss_a", align_bytes=64)
+        cs_q = keep.tile([P, NSET * Q_COLS], U32, name="cs_q", align_bytes=64)
+        ss_q = keep.tile([P, NSET * Q_COLS], U8, name="ss_q", align_bytes=64)
+        for t in (cs_a, ss_a, cs_q, ss_q):
+            nc.vector.memset(t[:].bitcast(I32)[32:64], 0)
 
         w_grp = keep.tile([P, 4, 256, 4], BF16, name="w_grp", align_bytes=64)
         wq = keep.tile([P, 4, 256], U32, name="wq", align_bytes=64)
         wqs = keep.tile([P, 4, 256], U8, name="wqs", align_bytes=64)
-        w1a = keep.tile([P, 256], U32, name="w1a", align_bytes=64)
-        w1b = keep.tile([P, 256], U32, name="w1b", align_bytes=64)
-        nc.vector.memset(w1a[:].bitcast(I32), 0)
-        nc.vector.memset(w1b[:].bitcast(I32), 0)
+        wa = keep.tile([P, 4, 256], U32, name="wa", align_bytes=64)
+        wb = keep.tile([P, 4, 256], U32, name="wb", align_bytes=64)
+        nc.vector.memset(wa[:].bitcast(I32), 0)
+        nc.vector.memset(wb[:].bitcast(I32), 0)
         perm = keep.tile([P, P], F32, name="perm")
         nc.vector.tensor_copy(
             out=perm[:].rearrange("p (w b) -> p w b", b=4),
@@ -119,18 +117,17 @@ def tile_qa_cnn_t_kernel(tc, question, answer, W, b, out_0, out_1):
                 scales=wqs[:, s, :],
                 in_=w_grp[:, s].rearrange("p c t -> p (c t)"),
             )
-            if s == 1:
-                nc.vector.tensor_copy(out=w1a[:].bitcast(I32)[0:96], in_=wq[:, 1, :].bitcast(I32)[0:96])
-                nc.vector.tensor_copy(
-                    out=w1b[:].bitcast(I32)[96:128], in_=wq[:, 1, :].bitcast(I32)[96:128]
-                )
+
+        def split_w(s):
+            whole = wq[:, s, :].bitcast(I32)
+            for dst, parts in ((wa, PLAIN_PARTS[s]), (wb, SHIFTED_PARTS[s])):
+                for lo, hi in parts:
+                    nc.vector.tensor_copy(out=dst[:, s, :].bitcast(I32)[lo:hi], in_=whole[lo:hi])
 
         def spread(src_c, src_s, dst_c, dst_s):
             for src, dst in ((src_c, dst_c), (src_s, dst_s)):
-                nc.vector.tensor_copy(out=dst[3], in_=src(0))
-                nc.vector.tensor_copy(out=dst[0][0:64], in_=src(0)[0:64])
-                nc.vector.tensor_copy(out=dst[0][64:128], in_=src(-1)[64:128])
-                nc.vector.tensor_copy(out=dst[3][0:32], in_=src(1)[0:32])
+                nc.vector.tensor_copy(out=dst[64:128], in_=src(-1)[64:128])
+                nc.vector.tensor_copy(out=dst[0:32], in_=src(1)[0:32])
 
         def turn_a(n):
             xw = xa[n][:].bitcast(F32)
@@ -170,11 +167,8 @@ def tile_qa_cnn_t_kernel(tc, question, answer, W, b, out_0, out_1):
             spread(
                 lambda d: c0_a_i[:, base + 4 * d : base + 4 * d + A_COLS],
                 lambda d: s0_a_i[:, base // 4 + d : base // 4 + d + A_COLS // 4],
-                dict((s, cs_a[s][:].bitcast(I32)[:, A_COLS * n : A_COLS * (n + 1)]) for s in MOVED),
-                dict(
-                    (s, ss_a[s][:].bitcast(I32)[:, A_COLS // 4 * n : A_COLS // 4 * (n + 1)])
-                    for s in MOVED
-                ),
+                cs_a[:].bitcast(I32)[:, A_COLS * n : A_COLS * (n + 1)],
+                ss_a[:].bitcast(I32)[:, A_COLS // 4 * n : A_COLS // 4 * (n + 1)],
             )
 
         def prep_a(n):
@@ -214,14 +208,8 @@ def tile_qa_cnn_t_kernel(tc, question, answer, W, b, out_0, out_1):
                 lambda d: s0_q_i[:, 16 + d : 16 + d + NSET * Q_PITCH // 4].rearrange(
                     "p (n c) -> p n c", c=Q_PITCH // 4
                 )[:, :, 0 : Q_COLS // 4],
-                dict(
-                    (s, cs_q[s][:].bitcast(I32).rearrange("p (n c) -> p n c", c=Q_COLS))
-                    for s in MOVED
-                ),
-                dict(
-                    (s, ss_q[s][:].bitcast(I32).rearrange("p (n c) -> p n c", c=Q_COLS // 4))
-                    for s in MOVED
-                ),
+                cs_q[:].bitcast(I32).rearrange("p (n c) -> p n c", c=Q_COLS),
+                ss_q[:].bitcast(I32).rearrange("p (n c) -> p n c", c=Q_COLS // 4),
             )
 
         def bank(h, on_vector, plain_c, plain_s, plain_at, moved_c, moved_s, moved_at, dest):
@@ -240,12 +228,11 @@ def tile_qa_cnn_t_kernel(tc, question, answer, W, b, out_0, out_1):
                 )
 
             one(2, wq[:, 2, cols], plain_c, plain_s, plain_at, True, True)
-            one(1, w1a[:, cols], plain_c, plain_s, plain_at, True, False)
-            one(1, w1b[:, cols], moved_c[0], moved_s[0], moved_at, False, True)
-            one(0, wq[:, 0, cols], moved_c[0], moved_s[0], moved_at, True, True)
-            one(3, wq[:, 3, cols], moved_c[3], moved_s[3], moved_at, True, True)
-            o_view = dest.rearrange("c b (u s) -> c u s b", s=4)
-            a_view = acc[:].rearrange("c s (u b) -> c u s b", b=4)
+            for s in (0, 1, 3):
+                one(s, wa[:, s, cols], plain_c, plain_s, plain_at, True, False)
+                one(s, wb[:, s, cols], moved_c, moved_s, moved_at, False, True)
+            o_view = dest.rearrange("c b (u s) -> c u b s", s=4)
+            a_view = acc[:].rearrange("c s (u b) -> c u b s", b=4)
             if on_vector:
                 nc.vector.tensor_scalar(
                     out=o_view, in0=a_view, scalar1=bias[:, h : h + 1], scalar2=None, op0=ADD
@@ -296,7 +283,10 @@ def tile_qa_cnn_t_kernel(tc, question, answer, W, b, out_0, out_1):
         t1 = turn_a(1)
         spread_a(0)
         quant_w(3)
+        split_w(0)
         quant_w(1)
+        split_w(3)
+        split_w(1)
         nc.vector.tensor_copy(out=bias[:], in_=b_bf[:])
         quant_a(1, group_a(t1))
         spread_a(1)

@@ -16,15 +16,15 @@ ADD = mybir.AluOpType.add
 MULT = mybir.AluOpType.mult
 
 P = 128
-NSET = 6
-A_COLS = 512
-A_PITCH = 576
-Q_COLS = 128
-Q_PITCH = 192
+NA = 6
+NQ = 3
+A_COLS = (4 + 2) * P
+Q_COLS = (2 + 2) * P
 PLAIN_PARTS = {0: ((0, 64),), 1: ((0, 96),), 3: ((32, 64), (64, 128))}
 SHIFTED_PARTS = {0: ((64, 128),), 1: ((96, 128),), 3: ((0, 32),)}
-VEC_A = {0: (3,), 1: (3,), 2: (3,), 3: (3,), 4: (3,), 5: (1, 3, 5, 7)}
-VEC_Q = (1, 3)
+NEIGHBOUR = {0: -P, 1: -P, 3: P}
+SLOT = {0: 0, 1: 1, 3: 2}
+VEC_BANKS = {"a": (1, 3, 4), "q": (1, 3)}
 
 
 def tile_qa_cnn_t_kernel(tc, question, answer, W, b, out_0, out_1):
@@ -37,78 +37,66 @@ def tile_qa_cnn_t_kernel(tc, question, answer, W, b, out_0, out_1):
         mm_ps = ctx.enter_context(tc.psum_pool(name="mm", bufs=6))
         ctx.enter_context(tc.manual_schedule())
 
-        a_rows = answer.flatten_outer_dims().rearrange(
-            "(n b w g) e -> n w b (g e)", n=NSET, b=4, g=4
-        )
+        a_rows = answer.flatten_outer_dims().rearrange("(n p g) e -> n p (g e)", n=NA, g=16)
+        q_rows = question.flatten_outer_dims().rearrange("(n p g) e -> n p (g e)", n=NQ, g=8)
         w_rows = W.rearrange("(p t) c -> p (t c)", t=4)
         xa = []
-        for n in range(NSET):
-            xa.append(keep.tile([P, 4, 512], BF16, name="xa%d" % n))
+        for n in range(NA):
+            xa.append(keep.tile([P, 2048], BF16, name="xa%d" % n))
+        xq = []
+        for n in range(NQ):
+            xq.append(keep.tile([P, 1024], BF16, name="xq%d" % n))
         w_raw = keep.tile([P, 4, 1024], BF16, name="w_raw")
-        nc.sync.dma_start(out=xa[0][:], in_=a_rows[0])
-        nc.sync.dma_start(out=w_raw[:, 2, :], in_=w_rows)
+        b_bf = keep.tile([P, 2], BF16, name="b_bf")
+        nc.sync.dma_start(out=xq[0][:], in_=q_rows[0])
+        nc.scalar.dma_start(out=w_raw[:, 2, :], in_=w_rows)
         for s in (0, 3, 1):
             rot = 32 * ((2 - s) % 4)
-            nc.scalar.dma_start(out=w_raw[0 : P - rot, s, :], in_=w_rows[rot:P, :])
-            nc.scalar.dma_start(out=w_raw[P - rot : P, s, :], in_=w_rows[0:rot, :])
-        b_bf = keep.tile([P, 2], BF16, name="b_bf")
+            eng = nc.sync if s == 3 else nc.scalar
+            eng.dma_start(out=w_raw[0 : P - rot, s, :], in_=w_rows[rot:P, :])
+            eng.dma_start(out=w_raw[P - rot : P, s, :], in_=w_rows[0:rot, :])
+        nc.sync.dma_start(out=xa[0][:], in_=a_rows[0])
         with nc.allow_non_contiguous_dma(reason="256 bias values, one to a partition"):
-            nc.scalar.dma_start(out=b_bf[:], in_=b.rearrange("(h c) -> c h", h=2))
-        for n in range(1, NSET):
+            nc.sync.dma_start(out=b_bf[:], in_=b.rearrange("(h c) -> c h", h=2))
+        nc.sync.dma_start(out=xa[1][:], in_=a_rows[1])
+        nc.sync.dma_start(out=xq[1][:], in_=q_rows[1])
+        for n in range(2, NA):
             nc.sync.dma_start(out=xa[n][:], in_=a_rows[n])
-        xq = keep.tile([P, NSET, 512], BF16, name="xq")
-        nc.sync.dma_start(
-            out=xq[:],
-            in_=question.flatten_outer_dims().rearrange("(n k g) e -> k n (g e)", n=NSET, g=4),
-        )
+        nc.sync.dma_start(out=xq[2][:], in_=q_rows[2])
 
+        wa = keep.tile([P, 3, 256], U32, name="wa", align_bytes=64)
+        wb = keep.tile([P, 3, 256], U32, name="wb", align_bytes=64)
         ident = keep.tile([P, P], F32, name="ident")
         make_identity(nc, ident[:])
 
-        c0_a = keep.tile([P, 7 * A_PITCH], U32, name="c0_a", align_bytes=64)
-        s0_a = keep.tile([P, 7 * A_PITCH], U8, name="s0_a", align_bytes=64)
-        c0_q = keep.tile([P, 7 * Q_PITCH], U32, name="c0_q", align_bytes=64)
-        s0_q = keep.tile([P, 7 * Q_PITCH], U8, name="s0_q", align_bytes=64)
-        c0_a_i = c0_a[:].bitcast(I32)
-        s0_a_i = s0_a[:].bitcast(I32)
-        c0_q_i = c0_q[:].bitcast(I32)
-        s0_q_i = s0_q[:].bitcast(I32)
-        nc.vector.memset(c0_a_i.rearrange("p (n c) -> p n c", c=A_PITCH)[:, :, 0:64], 0)
-        nc.vector.memset(s0_a_i, 0)
-        nc.vector.memset(c0_q_i.rearrange("p (n c) -> p n c", c=Q_PITCH)[:, :, 0:64], 0)
-        nc.vector.memset(s0_q_i, 0)
-        cs_a = keep.tile([P, NSET * A_COLS], U32, name="cs_a", align_bytes=64)
-        ss_a = keep.tile([P, NSET * A_COLS], U8, name="ss_a", align_bytes=64)
-        cs_q = keep.tile([P, NSET * Q_COLS], U32, name="cs_q", align_bytes=64)
-        ss_q = keep.tile([P, NSET * Q_COLS], U8, name="ss_q", align_bytes=64)
-        for t in (cs_a, ss_a, cs_q, ss_q):
-            nc.vector.memset(t[:].bitcast(I32)[32:64], 0)
+        c_a = keep.tile([P, NA * A_COLS], U32, name="c_a", align_bytes=64)
+        s_a = keep.tile([P, NA * A_COLS], U8, name="s_a", align_bytes=64)
+        c_q = keep.tile([P, NQ * Q_COLS], U32, name="c_q", align_bytes=64)
+        s_q = keep.tile([P, NQ * Q_COLS], U8, name="s_q", align_bytes=64)
+        for t in (s_q, wa, wb, s_a):
+            nc.gpsimd.memset(t[:].bitcast(I32), 0)
+        for codes, cols, lanes in ((c_q, Q_COLS, 16), (c_a, A_COLS, 32)):
+            v = codes[:].bitcast(I32).rearrange("p (n c) -> p n c", c=cols)
+            first = v[:, :, 0:P].rearrange("p n (b l) -> p n b l", l=lanes)
+            last = v[:, :, cols - P : cols].rearrange("p n (b l) -> p n b l", l=lanes)
+            nc.vector.memset(first[:, :, :, 0:1], 0)
+            nc.vector.memset(last[:, :, :, lanes - 1 : lanes], 0)
 
         w_grp = keep.tile([P, 4, 256, 4], BF16, name="w_grp", align_bytes=64)
         wq = keep.tile([P, 4, 256], U32, name="wq", align_bytes=64)
         wqs = keep.tile([P, 4, 256], U8, name="wqs", align_bytes=64)
-        wa = keep.tile([P, 4, 256], U32, name="wa", align_bytes=64)
-        wb = keep.tile([P, 4, 256], U32, name="wb", align_bytes=64)
-        nc.vector.memset(wa[:].bitcast(I32), 0)
-        nc.vector.memset(wb[:].bitcast(I32), 0)
-        perm = keep.tile([P, P], F32, name="perm")
-        nc.vector.tensor_copy(
-            out=perm[:].rearrange("p (w b) -> p w b", b=4),
-            in_=ident[:].rearrange("p (b w) -> p w b", b=4),
-        )
         bias = keep.tile([P, 2], F32, name="bias")
+        warm = keep.tile([P, 1], F32, name="warm")
 
-        def regroup_w():
-            for s in (2, 0):
-                nc.scalar.copy(out=w_grp[:, s], in_=w_raw[:, s, :].rearrange("p (t c) -> p c t", t=4))
-            for s in (3, 1):
+        def regroup_w(s, on):
+            src = w_raw[:, s, :].rearrange("p (t c) -> p c t", t=4)
+            if on == "v":
+                nc.vector.tensor_copy(out=w_grp[:, s], in_=src)
+            elif on == "s":
+                nc.scalar.copy(out=w_grp[:, s], in_=src)
+            else:
                 nc.gpsimd.tensor_scalar(
-                    out=w_grp[:, s],
-                    in0=w_raw[:, s, :].rearrange("p (t c) -> p c t", t=4),
-                    scalar1=1.0,
-                    scalar2=0.0,
-                    op0=MULT,
-                    op1=ADD,
+                    out=w_grp[:, s], in0=src, scalar1=1.0, scalar2=0.0, op0=MULT, op1=ADD
                 )
 
         def quant_w(s):
@@ -122,117 +110,89 @@ def tile_qa_cnn_t_kernel(tc, question, answer, W, b, out_0, out_1):
             whole = wq[:, s, :].bitcast(I32)
             for dst, parts in ((wa, PLAIN_PARTS[s]), (wb, SHIFTED_PARTS[s])):
                 for lo, hi in parts:
-                    nc.vector.tensor_copy(out=dst[:, s, :].bitcast(I32)[lo:hi], in_=whole[lo:hi])
+                    nc.vector.tensor_copy(out=dst[:, SLOT[s], :].bitcast(I32)[lo:hi], in_=whole[lo:hi])
 
-        def spread(src_c, src_s, dst_c, dst_s):
-            for src, dst in ((src_c, dst_c), (src_s, dst_s)):
-                nc.vector.tensor_copy(out=dst[64:128], in_=src(-1)[64:128])
-                nc.vector.tensor_copy(out=dst[0:32], in_=src(1)[0:32])
+        def geometry(unit):
+            kind, n = unit
+            if kind == "a":
+                return xa[n], c_a, s_a, A_COLS * n, 4, 32
+            return xq[n], c_q, s_q, Q_COLS * n, 2, 16
 
-        def turn_a(n):
-            xw = xa[n][:].bitcast(F32)
+        def turn(unit):
+            x, codes, planes, base, groups, lanes = geometry(unit)
+            xw = x[:].bitcast(F32)
             turned = []
-            for half in range(2):
+            for half in range(groups // 2):
                 tp = tp_ps.tile([P, 2, 2, P], F32, tag="tp")
                 turned.append(tp)
-                for bb in range(2):
+                for kk in range(2):
+                    k = 2 * half + kk
                     for u in range(2):
                         nc.tensor.transpose(
-                            tp[:, bb, u, :],
-                            xw[:, 2 * half + bb, :].rearrange("p (m u) -> p u m", u=2)[:, u, :],
+                            tp[:, kk, u, :],
+                            xw[:, 256 * k : 256 * k + 256].rearrange("p (m u) -> p u m", u=2)[:, u, :],
                             ident[:],
                         )
             return turned
 
-        def group_a(turned):
-            grouped = gpool.tile([P, 4 * A_COLS], BF16, tag="ga", align_bytes=64)
-            g32 = grouped[:].bitcast(F32).rearrange("p (w b u) -> p w b u", b=4, u=2)
-            for half in range(2):
-                nc.vector.tensor_copy(
-                    out=g32[:, :, 2 * half : 2 * half + 2, :],
-                    in_=turned[half][:].rearrange("p b u w -> p w b u"),
-                )
+        def group(unit, turned, on_scalar=False):
+            groups = geometry(unit)[4]
+            grouped = gpool.tile([P, groups * 512], BF16, tag="g" + unit[0], align_bytes=64)
+            g32 = grouped[:].bitcast(F32).rearrange("p (k w u) -> p k w u", w=P, u=2)
+            for half in range(groups // 2):
+                dst = g32[:, 2 * half : 2 * half + 2]
+                src = turned[half][:].rearrange("p k u w -> p k w u")
+                if on_scalar:
+                    nc.scalar.copy(out=dst, in_=src)
+                else:
+                    nc.vector.tensor_copy(out=dst, in_=src)
             return grouped
 
-        def quant_a(n, grouped):
-            base = 64 + A_PITCH * n
+        def quant(unit, grouped):
+            x, codes, planes, base, groups, lanes = geometry(unit)
+            lo, hi = base + P, base + P + P * groups
             nc.vector.quantize_mx(
-                out=c0_a[:, base : base + A_COLS].bitcast(FP8X4),
-                scales=s0_a[:, base : base + A_COLS],
-                in_=grouped[:],
+                out=codes[:, lo:hi].bitcast(FP8X4), scales=planes[:, lo:hi], in_=grouped[:]
             )
 
-        def spread_a(n):
-            base = 64 + A_PITCH * n
-            spread(
-                lambda d: c0_a_i[:, base + 4 * d : base + 4 * d + A_COLS],
-                lambda d: s0_a_i[:, base // 4 + d : base // 4 + d + A_COLS // 4],
-                cs_a[:].bitcast(I32)[:, A_COLS * n : A_COLS * (n + 1)],
-                ss_a[:].bitcast(I32)[:, A_COLS // 4 * n : A_COLS // 4 * (n + 1)],
-            )
+        def halo(unit):
+            x, codes, planes, base, groups, lanes = geometry(unit)
+            for t in (codes[:].bitcast(I32), planes[:]):
 
-        def prep_a(n):
-            quant_a(n, group_a(turn_a(n)))
-            spread_a(n)
+                def block(r):
+                    lo = base + P * (r + 1)
+                    return t[:, lo : lo + P].rearrange("p (b l) -> p b l", l=lanes)
 
-        def prep_q():
-            xw = xq[:].bitcast(F32)
-            tiles = []
-            for pair in range(NSET // 2):
-                grouped = gpool.tile([P, 2, 4 * Q_COLS], BF16, tag="gq", align_bytes=64)
-                tiles.append(grouped)
-                tp = tp_ps.tile([P, 2, 2, P], F32, tag="tp")
-                for bb in range(2):
-                    for u in range(2):
-                        nc.tensor.transpose(
-                            tp[:, bb, u, :],
-                            xw[:, 2 * pair + bb, :].rearrange("p (m u) -> p u m", u=2)[:, u, :],
-                            perm[:],
-                        )
                 nc.vector.tensor_copy(
-                    out=grouped[:].bitcast(F32).rearrange("p n (c u) -> p n c u", u=2),
-                    in_=tp[:].rearrange("p n u c -> p n c u"),
+                    out=block(-1)[:, :, 1:lanes], in_=block(groups - 1)[:, :, 0 : lanes - 1]
                 )
-            for pair in range(NSET // 2):
-                for bb in range(2):
-                    base = 64 + Q_PITCH * (2 * pair + bb)
-                    nc.vector.quantize_mx(
-                        out=c0_q[:, base : base + Q_COLS].bitcast(FP8X4),
-                        scales=s0_q[:, base : base + Q_COLS],
-                        in_=tiles[pair][:, bb, :],
-                    )
-            spread(
-                lambda d: c0_q_i[:, 64 + 4 * d : 64 + 4 * d + NSET * Q_PITCH].rearrange(
-                    "p (n c) -> p n c", c=Q_PITCH
-                )[:, :, 0:Q_COLS],
-                lambda d: s0_q_i[:, 16 + d : 16 + d + NSET * Q_PITCH // 4].rearrange(
-                    "p (n c) -> p n c", c=Q_PITCH // 4
-                )[:, :, 0 : Q_COLS // 4],
-                cs_q[:].bitcast(I32).rearrange("p (n c) -> p n c", c=Q_COLS),
-                ss_q[:].bitcast(I32).rearrange("p (n c) -> p n c", c=Q_COLS // 4),
-            )
+                nc.vector.tensor_copy(
+                    out=block(groups)[:, :, 0 : lanes - 1], in_=block(0)[:, :, 1:lanes]
+                )
 
-        def bank(h, on_vector, plain_c, plain_s, plain_at, moved_c, moved_s, moved_at, dest):
+        def bank(unit, h, r, on_vector, dest):
+            x, codes, planes, base, groups, lanes = geometry(unit)
+            at = base + P * (r + 1)
             acc = mm_ps.tile([P, 4, P], F32, tag="mm")
             cols = slice(P * h, P * h + P)
 
-            def one(s, weights, codes, planes, at, start, stop):
+            def one(s, weights, col, start, stop):
                 nc.tensor.matmul_mx(
                     out=acc[:, s, :],
                     lhsT=weights.bitcast(FP8X4),
                     lhsT_scale=wqs[:, s, cols],
-                    rhs=codes[:, at : at + P].bitcast(FP8X4),
-                    rhs_scale=planes[:, at : at + P],
+                    rhs=codes[:, col : col + P].bitcast(FP8X4),
+                    rhs_scale=planes[:, col : col + P],
                     start=start,
                     stop=stop,
                 )
 
-            one(2, wq[:, 2, cols], plain_c, plain_s, plain_at, True, True)
-            for s in (0, 1, 3):
-                one(s, wa[:, s, cols], plain_c, plain_s, plain_at, True, False)
-                one(s, wb[:, s, cols], moved_c, moved_s, moved_at, False, True)
-            o_view = dest.rearrange("c b (u s) -> c u b s", s=4)
-            a_view = acc[:].rearrange("c s (u b) -> c u b s", b=4)
+            one(2, wq[:, 2, cols], at, True, True)
+            for s in (0, 3, 1):
+                one(s, wa[:, SLOT[s], cols], at, True, False)
+                one(s, wb[:, SLOT[s], cols], at + NEIGHBOUR[s], False, True)
+            o_view = dest.rearrange("c (w r s) -> c w r s", r=groups, s=4)[:, :, r, :]
+            a_view = acc[:].rearrange("c s w -> c w s")
             if on_vector:
                 nc.vector.tensor_scalar(
                     out=o_view, in0=a_view, scalar1=bias[:, h : h + 1], scalar2=None, op0=ADD
@@ -242,59 +202,60 @@ def tile_qa_cnn_t_kernel(tc, question, answer, W, b, out_0, out_1):
                     out=o_view, in_=a_view, func=IDENTITY, bias=bias[:, h : h + 1], scale=1.0
                 )
 
-        def run_a(n, mid=None):
+        def run(unit, after):
+            kind, n = unit
+            groups = 4 if kind == "a" else 2
+            sentences, length = (4, 512) if kind == "a" else (8, 128)
+            dram = out_1 if kind == "a" else out_0
             for h in range(2):
-                o = opool.tile([P, 4, 512], F32, tag="oa")
-                for v in range(4):
-                    bank(
-                        h, (4 * h + v) in VEC_A[n],
-                        c0_a, s0_a, 64 + A_PITCH * n + P * v,
-                        cs_a, ss_a, A_COLS * n + P * v,
-                        o[:, :, P * v : P * v + P],
-                    )
+                o = opool.tile([P, sentences * length], F32, tag="o" + kind)
+                for r in range(groups):
+                    i = groups * h + r
+                    bank(unit, h, r, i in VEC_BANKS[kind], o[:])
+                    if i in after:
+                        after[i]()
                 nc.sync.dma_start(
-                    out=out_1[4 * n : 4 * n + 4, P * h : P * h + P, :].rearrange("b c i -> c b i"),
-                    in_=o[:],
-                )
-                if h == 0 and mid is not None:
-                    mid()
-
-        def run_q(pair):
-            for h in range(2):
-                o = opool.tile([P, 8, P], F32, tag="oq")
-                for bb in range(2):
-                    n = 2 * pair + bb
-                    bank(
-                        h, (2 * h + bb) in VEC_Q,
-                        c0_q, s0_q, 64 + Q_PITCH * n,
-                        cs_q, ss_q, Q_COLS * n,
-                        o[:, 4 * bb : 4 * bb + 4, :],
-                    )
-                nc.sync.dma_start(
-                    out=out_0[8 * pair : 8 * pair + 8, P * h : P * h + P, :].rearrange("b c i -> c b i"),
-                    in_=o[:],
+                    out=dram[sentences * n : sentences * n + sentences, P * h : P * h + P, :].rearrange(
+                        "b c i -> c b i"
+                    ),
+                    in_=o[:].rearrange("c (b i) -> c b i", i=length),
                 )
 
-        g0 = group_a(turn_a(0))
-        regroup_w()
-        quant_a(0, g0)
+        units = [("q", 0), ("a", 0), ("a", 1), ("q", 1), ("a", 2), ("a", 3), ("a", 4), ("a", 5), ("q", 2)]
+
+        nc.scalar.activation(out=warm[:], in_=ident[:, 0:1], func=IDENTITY, bias=0.0, scale=1.0)
+        t0 = turn(units[0])
+        regroup_w(2, "v")
+        g0 = group(units[0], t0, on_scalar=True)
+        regroup_w(1, "g")
+        regroup_w(0, "v")
+        t1 = turn(units[1])
+        quant(units[0], g0)
         quant_w(2)
         quant_w(0)
-        t1 = turn_a(1)
-        spread_a(0)
-        quant_w(3)
+        regroup_w(3, "s")
+        g1 = group(units[1], t1, on_scalar=True)
+        halo(units[0])
         split_w(0)
-        quant_w(1)
+        quant_w(3)
         split_w(3)
+        quant_w(1)
         split_w(1)
         nc.vector.tensor_copy(out=bias[:], in_=b_bf[:])
-        quant_a(1, group_a(t1))
-        spread_a(1)
-        run_a(0, lambda: prep_a(2))
-        run_a(1, lambda: prep_a(3))
-        run_a(2, lambda: prep_a(4))
-        run_a(3, lambda: prep_a(5))
-        run_a(4, prep_q)
-        run_a(5)
-        for pair in range(NSET // 2):
-            run_q(pair)
+        quant(units[1], g1)
+        halo(units[1])
+
+        def hooks(i):
+            if i + 2 >= len(units):
+                return {}
+            ahead = units[i + 2]
+            half = 4 if units[i][0] == "a" else 2
+            held = {}
+
+            def first():
+                held["g"] = group(ahead, turn(ahead))
+
+            return {half - 1: first, half: lambda: quant(ahead, held["g"]), half + 1: lambda: halo(ahead)}
+
+        for i in range(len(units)):
+            run(units[i], hooks(i))

@@ -20,11 +20,11 @@ NA = 6
 NQ = 3
 A_COLS = (4 + 2) * P
 Q_COLS = (2 + 2) * P
-PLAIN_PARTS = {0: ((0, 64),), 1: ((0, 96),), 3: ((32, 64), (64, 128))}
-SHIFTED_PARTS = {0: ((64, 128),), 1: ((96, 128),), 3: ((0, 32),)}
-NEIGHBOUR = {0: -P, 1: -P, 3: P}
-SLOT = {0: 0, 1: 1, 3: 2}
-VEC_BANKS = {"a": (1, 3, 4), "q": (1, 3)}
+PLAIN_PARTS = {1: ((0, 96),), 3: ((32, 64), (64, 128))}
+SHIFTED_PARTS = {1: ((96, 128),), 3: ((0, 32),)}
+NEIGHBOUR = {1: -P, 3: P}
+SLOT = {1: 0, 3: 1}
+VEC_BANKS = {"a": (1, 4), "q": (3,)}
 
 
 def tile_qa_cnn_t_kernel(tc, question, answer, W, b, out_0, out_1):
@@ -32,6 +32,7 @@ def tile_qa_cnn_t_kernel(tc, question, answer, W, b, out_0, out_1):
     with ExitStack() as ctx:
         keep = ctx.enter_context(tc.tile_pool(name="keep", bufs=1))
         gpool = ctx.enter_context(tc.tile_pool(name="grouped", bufs=3))
+        mpool = ctx.enter_context(tc.tile_pool(name="moved", bufs=3))
         opool = ctx.enter_context(tc.tile_pool(name="outs", bufs=4))
         tp_ps = ctx.enter_context(tc.psum_pool(name="tp", bufs=2))
         mm_ps = ctx.enter_context(tc.psum_pool(name="mm", bufs=6))
@@ -49,10 +50,10 @@ def tile_qa_cnn_t_kernel(tc, question, answer, W, b, out_0, out_1):
         w_raw = keep.tile([P, 4, 1024], BF16, name="w_raw")
         b_bf = keep.tile([P, 2], BF16, name="b_bf")
         nc.sync.dma_start(out=xq[0][:], in_=q_rows[0])
-        nc.scalar.dma_start(out=w_raw[:, 2, :], in_=w_rows)
-        for s in (0, 3, 1):
+        nc.sync.dma_start(out=w_raw[:, 2, :], in_=w_rows)
+        for s in (3, 1, 0):
             rot = 32 * ((2 - s) % 4)
-            eng = nc.sync if s == 3 else nc.scalar
+            eng = nc.scalar if s == 1 else nc.sync
             eng.dma_start(out=w_raw[0 : P - rot, s, :], in_=w_rows[rot:P, :])
             eng.dma_start(out=w_raw[P - rot : P, s, :], in_=w_rows[0:rot, :])
         nc.sync.dma_start(out=xa[0][:], in_=a_rows[0])
@@ -64,10 +65,13 @@ def tile_qa_cnn_t_kernel(tc, question, answer, W, b, out_0, out_1):
             nc.sync.dma_start(out=xa[n][:], in_=a_rows[n])
         nc.sync.dma_start(out=xq[2][:], in_=q_rows[2])
 
-        wa = keep.tile([P, 3, 256], U32, name="wa", align_bytes=64)
-        wb = keep.tile([P, 3, 256], U32, name="wb", align_bytes=64)
+        wa = keep.tile([P, 2, 256], U32, name="wa", align_bytes=64)
+        wb = keep.tile([P, 2, 256], U32, name="wb", align_bytes=64)
         ident = keep.tile([P, P], F32, name="ident")
         make_identity(nc, ident[:])
+        warm = keep.tile([P, 1], F32, name="warm")
+        nc.vector.memset(warm[:], 0.0)
+        nc.scalar.activation(out=warm[:], in_=warm[:], func=IDENTITY, bias=0.0, scale=1.0)
 
         c_a = keep.tile([P, NA * A_COLS], U32, name="c_a", align_bytes=64)
         s_a = keep.tile([P, NA * A_COLS], U8, name="s_a", align_bytes=64)
@@ -86,7 +90,6 @@ def tile_qa_cnn_t_kernel(tc, question, answer, W, b, out_0, out_1):
         wq = keep.tile([P, 4, 256], U32, name="wq", align_bytes=64)
         wqs = keep.tile([P, 4, 256], U8, name="wqs", align_bytes=64)
         bias = keep.tile([P, 2], F32, name="bias")
-        warm = keep.tile([P, 1], F32, name="warm")
 
         def regroup_w(s, on):
             src = w_raw[:, s, :].rearrange("p (t c) -> p c t", t=4)
@@ -170,27 +173,52 @@ def tile_qa_cnn_t_kernel(tc, question, answer, W, b, out_0, out_1):
                     out=block(groups)[:, :, 0 : lanes - 1], in_=block(0)[:, :, 1:lanes]
                 )
 
-        def bank(unit, h, r, on_vector, dest):
+        moved = {}
+
+        def move(unit):
+            x, codes, planes, base, groups, lanes = geometry(unit)
+            mc = mpool.tile([P, groups * P], U32, tag="mc" + unit[0], align_bytes=64)
+            ms = mpool.tile([P, groups * P], U8, tag="ms" + unit[0], align_bytes=64)
+            moved[unit] = (mc, ms)
+            for src, dst in ((codes, mc), (planes, ms)):
+                for lo, hi, back in ((64, 128, P), (0, 64, 0)):
+                    at = base + P - back
+                    nc.vector.tensor_copy(
+                        out=dst[:].bitcast(I32)[lo:hi],
+                        in_=src[:, at : at + P * groups].bitcast(I32)[lo:hi],
+                    )
+
+        def new_bank():
+            acc = mm_ps.tile([P, 4, P], F32, tag="mm")
+            return acc
+
+        def multiply(unit, h, r, acc, which):
             x, codes, planes, base, groups, lanes = geometry(unit)
             at = base + P * (r + 1)
-            acc = mm_ps.tile([P, 4, P], F32, tag="mm")
             cols = slice(P * h, P * h + P)
 
-            def one(s, weights, col, start, stop):
+            def one(s, weights, xc, xs, col, start, stop):
                 nc.tensor.matmul_mx(
                     out=acc[:, s, :],
                     lhsT=weights.bitcast(FP8X4),
                     lhsT_scale=wqs[:, s, cols],
-                    rhs=codes[:, col : col + P].bitcast(FP8X4),
-                    rhs_scale=planes[:, col : col + P],
+                    rhs=xc[:, col : col + P].bitcast(FP8X4),
+                    rhs_scale=xs[:, col : col + P],
                     start=start,
                     stop=stop,
                 )
 
-            one(2, wq[:, 2, cols], at, True, True)
-            for s in (0, 3, 1):
-                one(s, wa[:, SLOT[s], cols], at, True, False)
-                one(s, wb[:, SLOT[s], cols], at + NEIGHBOUR[s], False, True)
+            for s in which:
+                if s == 2:
+                    one(s, wq[:, s, cols], codes, planes, at, True, True)
+                elif s == 0:
+                    one(s, wq[:, s, cols], moved[unit][0], moved[unit][1], P * r, True, True)
+                else:
+                    one(s, wa[:, SLOT[s], cols], codes, planes, at, True, False)
+                    one(s, wb[:, SLOT[s], cols], codes, planes, at + NEIGHBOUR[s], False, True)
+
+        def empty(unit, h, r, acc, on_vector, dest):
+            groups = geometry(unit)[4]
             o_view = dest.rearrange("c (w r s) -> c w r s", r=groups, s=4)[:, :, r, :]
             a_view = acc[:].rearrange("c s w -> c w s")
             if on_vector:
@@ -202,48 +230,75 @@ def tile_qa_cnn_t_kernel(tc, question, answer, W, b, out_0, out_1):
                     out=o_view, in_=a_view, func=IDENTITY, bias=bias[:, h : h + 1], scale=1.0
                 )
 
-        def run(unit, after):
+        def store(unit, h, o):
             kind, n = unit
-            groups = 4 if kind == "a" else 2
             sentences, length = (4, 512) if kind == "a" else (8, 128)
             dram = out_1 if kind == "a" else out_0
+            nc.sync.dma_start(
+                out=dram[sentences * n : sentences * n + sentences, P * h : P * h + P, :].rearrange(
+                    "b c i -> c b i"
+                ),
+                in_=o[:].rearrange("c (b i) -> c b i", i=length),
+            )
+
+        def out_tile(unit):
+            o = opool.tile([P, 512 * geometry(unit)[4]], F32, tag="o" + unit[0])
+            return o
+
+        def run(unit, after):
+            kind = unit[0]
+            groups = geometry(unit)[4]
             for h in range(2):
-                o = opool.tile([P, sentences * length], F32, tag="o" + kind)
+                o = out_tile(unit)
                 for r in range(groups):
                     i = groups * h + r
-                    bank(unit, h, r, i in VEC_BANKS[kind], o[:])
+                    acc = new_bank()
+                    multiply(unit, h, r, acc, (2, 3, 1, 0))
+                    empty(unit, h, r, acc, i in VEC_BANKS[kind], o[:])
                     if i in after:
                         after[i]()
-                nc.sync.dma_start(
-                    out=dram[sentences * n : sentences * n + sentences, P * h : P * h + P, :].rearrange(
-                        "b c i -> c b i"
-                    ),
-                    in_=o[:].rearrange("c (b i) -> c b i", i=length),
-                )
+                store(unit, h, o)
 
         units = [("q", 0), ("a", 0), ("a", 1), ("q", 1), ("a", 2), ("a", 3), ("a", 4), ("a", 5), ("q", 2)]
 
-        nc.scalar.activation(out=warm[:], in_=ident[:, 0:1], func=IDENTITY, bias=0.0, scale=1.0)
         t0 = turn(units[0])
         regroup_w(2, "v")
         g0 = group(units[0], t0, on_scalar=True)
         regroup_w(1, "g")
-        regroup_w(0, "v")
-        t1 = turn(units[1])
-        quant(units[0], g0)
         quant_w(2)
-        quant_w(0)
         regroup_w(3, "s")
-        g1 = group(units[1], t1, on_scalar=True)
+        quant(units[0], g0)
         halo(units[0])
-        split_w(0)
+        move(units[0])
         quant_w(3)
         split_w(3)
         quant_w(1)
         split_w(1)
+        regroup_w(0, "v")
+        quant_w(0)
         nc.vector.tensor_copy(out=bias[:], in_=b_bf[:])
+        head = [(h, r, new_bank()) for h in range(2) for r in range(2)]
+        for h, r, acc in head:
+            multiply(units[0], h, r, acc, (2,))
+        t1 = turn(units[1])
+        g1 = group(units[1], t1, on_scalar=True)
+        for s in (3, 1, 0):
+            for h, r, acc in head:
+                multiply(units[0], h, r, acc, (s,))
         quant(units[1], g1)
         halo(units[1])
+        move(units[1])
+        t2 = turn(units[2])
+        for h in range(2):
+            o = out_tile(units[0])
+            for r in range(2):
+                i = 2 * h + r
+                empty(units[0], h, r, head[i][2], i in VEC_BANKS["q"], o[:])
+            store(units[0], h, o)
+        g2 = group(units[2], t2)
+        quant(units[2], g2)
+        halo(units[2])
+        move(units[2])
 
         def hooks(i):
             if i + 2 >= len(units):
@@ -255,7 +310,11 @@ def tile_qa_cnn_t_kernel(tc, question, answer, W, b, out_0, out_1):
             def first():
                 held["g"] = group(ahead, turn(ahead))
 
-            return {half - 1: first, half: lambda: quant(ahead, held["g"]), half + 1: lambda: halo(ahead)}
+            def third():
+                halo(ahead)
+                move(ahead)
 
-        for i in range(len(units)):
+            return {half - 1: first, half: lambda: quant(ahead, held["g"]), half + 1: third}
+
+        for i in range(1, len(units)):
             run(units[i], hooks(i))

@@ -33,7 +33,7 @@ def tile_qa_cnn_t_kernel(tc, question, answer, W, b, out_0, out_1):
         keep = ctx.enter_context(tc.tile_pool(name="keep", bufs=1))
         gpool = ctx.enter_context(tc.tile_pool(name="grouped", bufs=3))
         mpool = ctx.enter_context(tc.tile_pool(name="moved", bufs=3))
-        opool = ctx.enter_context(tc.tile_pool(name="outs", bufs=4))
+        opool = ctx.enter_context(tc.tile_pool(name="outs", bufs=3))
         tp_ps = ctx.enter_context(tc.psum_pool(name="tp", bufs=2))
         mm_ps = ctx.enter_context(tc.psum_pool(name="mm", bufs=6))
         ctx.enter_context(tc.manual_schedule())
@@ -58,7 +58,7 @@ def tile_qa_cnn_t_kernel(tc, question, answer, W, b, out_0, out_1):
             eng.dma_start(out=w_raw[P - rot : P, s, :], in_=w_rows[0:rot, :])
         nc.sync.dma_start(out=xa[0][:], in_=a_rows[0])
         with nc.allow_non_contiguous_dma(reason="256 bias values, one to a partition"):
-            nc.sync.dma_start(out=b_bf[:], in_=b.rearrange("(h c) -> c h", h=2))
+            nc.sync.dma_start(out=b_bf[:], in_=b.rearrange("(c h) -> c h", h=2))
         nc.sync.dma_start(out=xa[1][:], in_=a_rows[1])
         nc.sync.dma_start(out=xq[1][:], in_=q_rows[1])
         for n in range(2, NA):
@@ -92,14 +92,15 @@ def tile_qa_cnn_t_kernel(tc, question, answer, W, b, out_0, out_1):
         bias = keep.tile([P, 2], F32, name="bias")
 
         def regroup_w(s, on):
-            src = w_raw[:, s, :].rearrange("p (t c) -> p c t", t=4)
+            src = w_raw[:, s, :].rearrange("p (t m h) -> p h m t", t=4, h=2)
+            dst = w_grp[:, s].rearrange("p (h m) t -> p h m t", h=2)
             if on == "v":
-                nc.vector.tensor_copy(out=w_grp[:, s], in_=src)
+                nc.vector.tensor_copy(out=dst, in_=src)
             elif on == "s":
-                nc.scalar.copy(out=w_grp[:, s], in_=src)
+                nc.scalar.copy(out=dst, in_=src)
             else:
                 nc.gpsimd.tensor_scalar(
-                    out=w_grp[:, s], in0=src, scalar1=1.0, scalar2=0.0, op0=MULT, op1=ADD
+                    out=dst, in0=src, scalar1=1.0, scalar2=0.0, op0=MULT, op1=ADD
                 )
 
         def quant_w(s):
@@ -218,9 +219,9 @@ def tile_qa_cnn_t_kernel(tc, question, answer, W, b, out_0, out_1):
                     one(s, wb[:, SLOT[s], cols], codes, planes, at + NEIGHBOUR[s], False, True)
 
         def empty(unit, h, r, acc, on_vector, dest):
-            groups = geometry(unit)[4]
-            o_view = dest.rearrange("c (w r s) -> c w r s", r=groups, s=4)[:, :, r, :]
-            a_view = acc[:].rearrange("c s w -> c w s")
+            groups, lanes = geometry(unit)[4:6]
+            o_view = dest[:, :, h, :].rearrange("c b (l r s) -> c b l r s", r=groups, s=4)[:, :, :, r, :]
+            a_view = acc[:].rearrange("c s (b l) -> c b l s", l=lanes)
             if on_vector:
                 nc.vector.tensor_scalar(
                     out=o_view, in0=a_view, scalar1=bias[:, h : h + 1], scalar2=None, op0=ADD
@@ -230,26 +231,27 @@ def tile_qa_cnn_t_kernel(tc, question, answer, W, b, out_0, out_1):
                     out=o_view, in_=a_view, func=IDENTITY, bias=bias[:, h : h + 1], scale=1.0
                 )
 
-        def store(unit, h, o):
+        def store(unit, o):
             kind, n = unit
-            sentences, length = (4, 512) if kind == "a" else (8, 128)
+            sentences = 4 if kind == "a" else 8
             dram = out_1 if kind == "a" else out_0
             nc.sync.dma_start(
-                out=dram[sentences * n : sentences * n + sentences, P * h : P * h + P, :].rearrange(
-                    "b c i -> c b i"
+                out=dram[sentences * n : sentences * n + sentences].rearrange(
+                    "b (c h) i -> c b (h i)", h=2
                 ),
-                in_=o[:].rearrange("c (b i) -> c b i", i=length),
+                in_=o[:].rearrange("c b h i -> c b (h i)"),
             )
 
         def out_tile(unit):
-            o = opool.tile([P, 512 * geometry(unit)[4]], F32, tag="o" + unit[0])
+            sentences, length = (4, 512) if unit[0] == "a" else (8, 128)
+            o = opool.tile([P, sentences, 2, length], F32, tag="o" + unit[0])
             return o
 
         def run(unit, after):
             kind = unit[0]
             groups = geometry(unit)[4]
+            o = out_tile(unit)
             for h in range(2):
-                o = out_tile(unit)
                 for r in range(groups):
                     i = groups * h + r
                     acc = new_bank()
@@ -257,7 +259,7 @@ def tile_qa_cnn_t_kernel(tc, question, answer, W, b, out_0, out_1):
                     empty(unit, h, r, acc, i in VEC_BANKS[kind], o[:])
                     if i in after:
                         after[i]()
-                store(unit, h, o)
+            store(unit, o)
 
         units = [("q", 0), ("a", 0), ("a", 1), ("q", 1), ("a", 2), ("a", 3), ("a", 4), ("a", 5), ("q", 2)]
 
@@ -289,12 +291,11 @@ def tile_qa_cnn_t_kernel(tc, question, answer, W, b, out_0, out_1):
         halo(units[1])
         move(units[1])
         t2 = turn(units[2])
-        for h in range(2):
-            o = out_tile(units[0])
-            for r in range(2):
-                i = 2 * h + r
-                empty(units[0], h, r, head[i][2], i in VEC_BANKS["q"], o[:])
-            store(units[0], h, o)
+        o = out_tile(units[0])
+        for i in range(4):
+            h, r, acc = head[i]
+            empty(units[0], h, r, acc, i in VEC_BANKS["q"], o[:])
+        store(units[0], o)
         g2 = group(units[2], t2)
         quant(units[2], g2)
         halo(units[2])

@@ -16,13 +16,12 @@ ADD = mybir.AluOpType.add
 MULT = mybir.AluOpType.mult
 
 P = 128
-NA = 6
-NQ = 3
-A_COLS = (4 + 2) * P
-Q_COLS = (2 + 2) * P
+L = 64
+WIDE = 4 * L
+KIND = {"a": (6, 2, 64), "q": (3, 1, 16)}
 PLAIN_PARTS = {1: ((0, 96),), 3: ((32, 64), (64, 128))}
 SHIFTED_PARTS = {1: ((96, 128),), 3: ((0, 32),)}
-NEIGHBOUR = {1: -P, 3: P}
+NEIGHBOUR = {1: -L, 3: L}
 SLOT = {1: 0, 3: 1}
 VEC_BANKS = {"a": (1, 4), "q": (3,)}
 
@@ -33,20 +32,20 @@ def tile_qa_cnn_t_kernel(tc, question, answer, W, b, out_0, out_1):
         keep = ctx.enter_context(tc.tile_pool(name="keep", bufs=1))
         gpool = ctx.enter_context(tc.tile_pool(name="grouped", bufs=3))
         mpool = ctx.enter_context(tc.tile_pool(name="moved", bufs=3))
-        opool = ctx.enter_context(tc.tile_pool(name="outs", bufs=3))
+        opool = ctx.enter_context(tc.tile_pool(name="outs", bufs=8))
         tp_ps = ctx.enter_context(tc.psum_pool(name="tp", bufs=2))
         mm_ps = ctx.enter_context(tc.psum_pool(name="mm", bufs=6))
         ctx.enter_context(tc.manual_schedule())
 
-        a_rows = answer.flatten_outer_dims().rearrange("(n p g) e -> n p (g e)", n=NA, g=16)
-        q_rows = question.flatten_outer_dims().rearrange("(n p g) e -> n p (g e)", n=NQ, g=8)
+        a_rows = answer.flatten_outer_dims().rearrange("(n k p g) e -> n p k (g e)", n=6, k=2, g=8)
+        q_rows = question.flatten_outer_dims().rearrange("(n k p g) e -> n p k (g e)", n=3, k=1, g=8)
         w_rows = W.rearrange("(p t) c -> p (t c)", t=4)
         xa = []
-        for n in range(NA):
-            xa.append(keep.tile([P, 2048], BF16, name="xa%d" % n))
+        for n in range(6):
+            xa.append(keep.tile([P, 2, 1024], BF16, name="xa%d" % n))
         xq = []
-        for n in range(NQ):
-            xq.append(keep.tile([P, 1024], BF16, name="xq%d" % n))
+        for n in range(3):
+            xq.append(keep.tile([P, 1, 1024], BF16, name="xq%d" % n))
         w_raw = keep.tile([P, 4, 1024], BF16, name="w_raw")
         b_bf = keep.tile([P, 2], BF16, name="b_bf")
         nc.sync.dma_start(out=xq[0][:], in_=q_rows[0])
@@ -57,11 +56,11 @@ def tile_qa_cnn_t_kernel(tc, question, answer, W, b, out_0, out_1):
             eng.dma_start(out=w_raw[0 : P - rot, s, :], in_=w_rows[rot:P, :])
             eng.dma_start(out=w_raw[P - rot : P, s, :], in_=w_rows[0:rot, :])
         nc.sync.dma_start(out=xa[0][:], in_=a_rows[0])
-        with nc.allow_non_contiguous_dma(reason="256 bias values, one to a partition"):
+        with nc.allow_non_contiguous_dma(reason="256 bias values, two to a partition"):
             nc.sync.dma_start(out=b_bf[:], in_=b.rearrange("(c h) -> c h", h=2))
         nc.sync.dma_start(out=xa[1][:], in_=a_rows[1])
         nc.sync.dma_start(out=xq[1][:], in_=q_rows[1])
-        for n in range(2, NA):
+        for n in range(2, 6):
             nc.sync.dma_start(out=xa[n][:], in_=a_rows[n])
         nc.sync.dma_start(out=xq[2][:], in_=q_rows[2])
 
@@ -73,18 +72,22 @@ def tile_qa_cnn_t_kernel(tc, question, answer, W, b, out_0, out_1):
         nc.vector.memset(warm[:], 0.0)
         nc.scalar.activation(out=warm[:], in_=warm[:], func=IDENTITY, bias=0.0, scale=1.0)
 
-        c_a = keep.tile([P, NA * A_COLS], U32, name="c_a", align_bytes=64)
-        s_a = keep.tile([P, NA * A_COLS], U8, name="s_a", align_bytes=64)
-        c_q = keep.tile([P, NQ * Q_COLS], U32, name="c_q", align_bytes=64)
-        s_q = keep.tile([P, NQ * Q_COLS], U8, name="s_q", align_bytes=64)
+        c_a = keep.tile([P, 24 * WIDE], U32, name="c_a", align_bytes=64)
+        s_a = keep.tile([P, 24 * WIDE], U8, name="s_a", align_bytes=64)
+        c_q = keep.tile([P, 6 * WIDE], U32, name="c_q", align_bytes=64)
+        s_q = keep.tile([P, 6 * WIDE], U8, name="s_q", align_bytes=64)
+        store_of = {"a": (c_a, s_a), "q": (c_q, s_q)}
+
+        def in_lanes(ap, kind):
+            return ap.rearrange("p (b k q l) -> p b k q l", k=4, l=KIND[kind][2], q=L // KIND[kind][2])
+
         for t in (s_q, wa, wb, s_a):
             nc.gpsimd.memset(t[:].bitcast(I32), 0)
-        for codes, cols, lanes in ((c_q, Q_COLS, 16), (c_a, A_COLS, 32)):
-            v = codes[:].bitcast(I32).rearrange("p (n c) -> p n c", c=cols)
-            first = v[:, :, 0:P].rearrange("p n (b l) -> p n b l", l=lanes)
-            last = v[:, :, cols - P : cols].rearrange("p n (b l) -> p n b l", l=lanes)
-            nc.vector.memset(first[:, :, :, 0:1], 0)
-            nc.vector.memset(last[:, :, :, lanes - 1 : lanes], 0)
+        for kind in ("q", "a"):
+            v = in_lanes(store_of[kind][0][:].bitcast(I32), kind)
+            last = KIND[kind][2] - 1
+            nc.vector.memset(v[:, :, 0, :, 0:1], 0)
+            nc.vector.memset(v[:, :, 3, :, last : last + 1], 0)
 
         w_grp = keep.tile([P, 4, 256, 4], BF16, name="w_grp", align_bytes=64)
         wq = keep.tile([P, 4, 256], U32, name="wq", align_bytes=64)
@@ -116,86 +119,84 @@ def tile_qa_cnn_t_kernel(tc, question, answer, W, b, out_0, out_1):
                 for lo, hi in parts:
                     nc.vector.tensor_copy(out=dst[:, SLOT[s], :].bitcast(I32)[lo:hi], in_=whole[lo:hi])
 
-        def geometry(unit):
-            kind, n = unit
-            if kind == "a":
-                return xa[n], c_a, s_a, A_COLS * n, 4, 32
-            return xq[n], c_q, s_q, Q_COLS * n, 2, 16
+        def pairs_of(unit):
+            return KIND[unit[0]][1]
+
+        def blocks_of(unit):
+            first = 2 * pairs_of(unit) * unit[1]
+            return range(first, first + 2 * pairs_of(unit))
+
+        def span(unit):
+            blocks = blocks_of(unit)
+            return slice(WIDE * blocks[0], WIDE * (blocks[0] + len(blocks)))
 
         def turn(unit):
-            x, codes, planes, base, groups, lanes = geometry(unit)
+            x = (xa if unit[0] == "a" else xq)[unit[1]]
             xw = x[:].bitcast(F32)
             turned = []
-            for half in range(groups // 2):
+            for k in range(pairs_of(unit)):
                 tp = tp_ps.tile([P, 2, 2, P], F32, tag="tp")
                 turned.append(tp)
-                for kk in range(2):
-                    k = 2 * half + kk
+                for r in range(2):
                     for u in range(2):
                         nc.tensor.transpose(
-                            tp[:, kk, u, :],
-                            xw[:, 256 * k : 256 * k + 256].rearrange("p (m u) -> p u m", u=2)[:, u, :],
+                            tp[:, r, u, :],
+                            xw[:, k, 256 * r : 256 * r + 256].rearrange("p (m u) -> p u m", u=2)[:, u, :],
                             ident[:],
                         )
             return turned
 
         def group(unit, turned, on_scalar=False):
-            groups = geometry(unit)[4]
-            grouped = gpool.tile([P, groups * 512], BF16, tag="g" + unit[0], align_bytes=64)
-            g32 = grouped[:].bitcast(F32).rearrange("p (k w u) -> p k w u", w=P, u=2)
-            for half in range(groups // 2):
-                dst = g32[:, 2 * half : 2 * half + 2]
-                src = turned[half][:].rearrange("p k u w -> p k w u")
-                if on_scalar:
-                    nc.scalar.copy(out=dst, in_=src)
-                else:
-                    nc.vector.tensor_copy(out=dst, in_=src)
+            pairs = pairs_of(unit)
+            grouped = gpool.tile([P, pairs * 2, 512], BF16, tag="g" + unit[0], align_bytes=64)
+            g32 = grouped[:].bitcast(F32).rearrange("p b (r l u) -> p b r l u", r=2, u=2)
+            for k in range(pairs):
+                src = turned[k][:].rearrange("p r u (b l) -> p b r l u", b=2)
+                for j in range(2):
+                    if on_scalar:
+                        nc.scalar.copy(out=g32[:, 2 * k + j], in_=src[:, j])
+                    else:
+                        nc.vector.tensor_copy(out=g32[:, 2 * k + j], in_=src[:, j])
             return grouped
 
         def quant(unit, grouped):
-            x, codes, planes, base, groups, lanes = geometry(unit)
-            lo, hi = base + P, base + P + P * groups
-            nc.vector.quantize_mx(
-                out=codes[:, lo:hi].bitcast(FP8X4), scales=planes[:, lo:hi], in_=grouped[:]
-            )
+            codes, planes = store_of[unit[0]]
+            for i, blk in enumerate(blocks_of(unit)):
+                lo = WIDE * blk + L
+                nc.vector.quantize_mx(
+                    out=codes[:, lo : lo + P].bitcast(FP8X4),
+                    scales=planes[:, lo : lo + P],
+                    in_=grouped[:, i, :],
+                )
 
         def halo(unit):
-            x, codes, planes, base, groups, lanes = geometry(unit)
-            for t in (codes[:].bitcast(I32), planes[:]):
-
-                def block(r):
-                    lo = base + P * (r + 1)
-                    return t[:, lo : lo + P].rearrange("p (b l) -> p b l", l=lanes)
-
-                nc.vector.tensor_copy(
-                    out=block(-1)[:, :, 1:lanes], in_=block(groups - 1)[:, :, 0 : lanes - 1]
-                )
-                nc.vector.tensor_copy(
-                    out=block(groups)[:, :, 0 : lanes - 1], in_=block(0)[:, :, 1:lanes]
-                )
+            codes, planes = store_of[unit[0]]
+            last = KIND[unit[0]][2] - 1
+            for ap in (codes[:, span(unit)].bitcast(I32), planes[:, span(unit)]):
+                v = in_lanes(ap, unit[0])
+                nc.vector.tensor_copy(out=v[:, :, 0, :, 1 : last + 1], in_=v[:, :, 2, :, 0:last])
+                nc.vector.tensor_copy(out=v[:, :, 3, :, 0:last], in_=v[:, :, 1, :, 1 : last + 1])
 
         moved = {}
 
         def move(unit):
-            x, codes, planes, base, groups, lanes = geometry(unit)
-            mc = mpool.tile([P, groups * P], U32, tag="mc" + unit[0], align_bytes=64)
-            ms = mpool.tile([P, groups * P], U8, tag="ms" + unit[0], align_bytes=64)
+            n = len(blocks_of(unit))
+            mc = mpool.tile([P, n * P], U32, tag="mc" + unit[0], align_bytes=64)
+            ms = mpool.tile([P, n * P], U8, tag="ms" + unit[0], align_bytes=64)
             moved[unit] = (mc, ms)
-            for src, dst in ((codes, mc), (planes, ms)):
-                for lo, hi, back in ((64, 128, P), (0, 64, 0)):
-                    at = base + P - back
-                    nc.vector.tensor_copy(
-                        out=dst[:].bitcast(I32)[lo:hi],
-                        in_=src[:, at : at + P * groups].bitcast(I32)[lo:hi],
-                    )
+            for src, dst, each in ((store_of[unit[0]][0], mc, 1), (store_of[unit[0]][1], ms, 4)):
+                v = src[:, span(unit)].bitcast(I32).rearrange("p (b w) -> p b w", w=WIDE // each)
+                d = dst[:].bitcast(I32).rearrange("p (b w) -> p b w", w=P // each)
+                for lo, hi, at in ((64, 128, 0), (0, 64, L // each)):
+                    nc.vector.tensor_copy(out=d[lo:hi], in_=v[lo:hi, :, at : at + P // each])
 
         def new_bank():
             acc = mm_ps.tile([P, 4, P], F32, tag="mm")
             return acc
 
-        def multiply(unit, h, r, acc, which):
-            x, codes, planes, base, groups, lanes = geometry(unit)
-            at = base + P * (r + 1)
+        def multiply(unit, i, h, acc, which):
+            codes, planes = store_of[unit[0]]
+            at = WIDE * blocks_of(unit)[i] + L
             cols = slice(P * h, P * h + P)
 
             def one(s, weights, xc, xs, col, start, stop):
@@ -213,15 +214,18 @@ def tile_qa_cnn_t_kernel(tc, question, answer, W, b, out_0, out_1):
                 if s == 2:
                     one(s, wq[:, s, cols], codes, planes, at, True, True)
                 elif s == 0:
-                    one(s, wq[:, s, cols], moved[unit][0], moved[unit][1], P * r, True, True)
+                    one(s, wq[:, s, cols], moved[unit][0], moved[unit][1], P * i, True, True)
                 else:
                     one(s, wa[:, SLOT[s], cols], codes, planes, at, True, False)
                     one(s, wb[:, SLOT[s], cols], codes, planes, at + NEIGHBOUR[s], False, True)
 
-        def empty(unit, h, r, acc, on_vector, dest):
-            groups, lanes = geometry(unit)[4:6]
-            o_view = dest[:, :, h, :].rearrange("c b (l r s) -> c b l r s", r=groups, s=4)[:, :, :, r, :]
-            a_view = acc[:].rearrange("c s (b l) -> c b l s", l=lanes)
+        def empty(unit, h, acc, on_vector, o):
+            if unit[0] == "a":
+                o_view = o.rearrange("c (h l r s) -> c h r l s", h=2, r=2, s=4)[:, h]
+                a_view = acc[:].rearrange("c s (r l) -> c r l s", r=2)
+            else:
+                o_view = o.rearrange("c (b h l r s) -> c h b l r s", b=4, h=2, r=2, s=4)[:, h]
+                a_view = acc[:].rearrange("c s (r b l) -> c b l r s", r=2, b=4)
             if on_vector:
                 nc.vector.tensor_scalar(
                     out=o_view, in0=a_view, scalar1=bias[:, h : h + 1], scalar2=None, op0=ADD
@@ -231,35 +235,30 @@ def tile_qa_cnn_t_kernel(tc, question, answer, W, b, out_0, out_1):
                     out=o_view, in_=a_view, func=IDENTITY, bias=bias[:, h : h + 1], scale=1.0
                 )
 
-        def store(unit, o):
-            kind, n = unit
-            sentences = 4 if kind == "a" else 8
-            dram = out_1 if kind == "a" else out_0
-            nc.sync.dma_start(
-                out=dram[sentences * n : sentences * n + sentences].rearrange(
-                    "b (c h) i -> c b (h i)", h=2
-                ),
-                in_=o[:].rearrange("c b h i -> c b (h i)"),
-            )
-
-        def out_tile(unit):
-            sentences, length = (4, 512) if unit[0] == "a" else (8, 128)
-            o = opool.tile([P, sentences, 2, length], F32, tag="o" + unit[0])
+        def out_tile():
+            o = opool.tile([P, 1024], F32, tag="o")
             return o
 
+        def store(unit, i, o):
+            blk = blocks_of(unit)[i]
+            if unit[0] == "a":
+                nc.sync.dma_start(out=out_1[blk].rearrange("(c h) i -> c (h i)", h=2), in_=o[:])
+            else:
+                nc.sync.dma_start(
+                    out=out_0[4 * blk : 4 * blk + 4].rearrange("b (c h) i -> c b (h i)", h=2),
+                    in_=o[:].rearrange("c (b f) -> c b f", b=4),
+                )
+
         def run(unit, after):
-            kind = unit[0]
-            groups = geometry(unit)[4]
-            o = out_tile(unit)
-            for h in range(2):
-                for r in range(groups):
-                    i = groups * h + r
+            for i in range(len(blocks_of(unit))):
+                o = out_tile()
+                for h in range(2):
                     acc = new_bank()
-                    multiply(unit, h, r, acc, (2, 3, 1, 0))
-                    empty(unit, h, r, acc, i in VEC_BANKS[kind], o[:])
-                    if i in after:
-                        after[i]()
-            store(unit, o)
+                    multiply(unit, i, h, acc, (2, 3, 1, 0))
+                    empty(unit, h, acc, 2 * i + h in VEC_BANKS[unit[0]], o[:])
+                    if 2 * i + h in after:
+                        after[2 * i + h]()
+                store(unit, i, o)
 
         units = [("q", 0), ("a", 0), ("a", 1), ("q", 1), ("a", 2), ("a", 3), ("a", 4), ("a", 5), ("q", 2)]
 
@@ -279,23 +278,23 @@ def tile_qa_cnn_t_kernel(tc, question, answer, W, b, out_0, out_1):
         regroup_w(0, "v")
         quant_w(0)
         nc.vector.tensor_copy(out=bias[:], in_=b_bf[:])
-        head = [(h, r, new_bank()) for h in range(2) for r in range(2)]
-        for h, r, acc in head:
-            multiply(units[0], h, r, acc, (2,))
+        head = [(i, h, new_bank()) for i in range(2) for h in range(2)]
+        for i, h, acc in head:
+            multiply(units[0], i, h, acc, (2,))
         t1 = turn(units[1])
         g1 = group(units[1], t1, on_scalar=True)
         for s in (3, 1, 0):
-            for h, r, acc in head:
-                multiply(units[0], h, r, acc, (s,))
+            for i, h, acc in head:
+                multiply(units[0], i, h, acc, (s,))
         quant(units[1], g1)
         halo(units[1])
         move(units[1])
         t2 = turn(units[2])
-        o = out_tile(units[0])
-        for i in range(4):
-            h, r, acc = head[i]
-            empty(units[0], h, r, acc, i in VEC_BANKS["q"], o[:])
-        store(units[0], o)
+        for i in range(2):
+            o = out_tile()
+            for h in range(2):
+                empty(units[0], h, head[2 * i + h][2], 2 * i + h in VEC_BANKS["q"], o[:])
+            store(units[0], i, o)
         g2 = group(units[2], t2)
         quant(units[2], g2)
         halo(units[2])

@@ -23,7 +23,7 @@ PLAIN_PARTS = {1: ((0, 96),), 3: ((32, 64), (64, 128))}
 SHIFTED_PARTS = {1: ((96, 128),), 3: ((0, 32),)}
 NEIGHBOUR = {1: -L, 3: L}
 SLOT = {1: 0, 3: 1}
-VEC_BANKS = {"a": (1, 4), "q": (3,)}
+VEC_BANKS = {"a": (), "q": ()}
 
 
 def tile_qa_cnn_t_kernel(tc, question, answer, W, b, out_0, out_1):
@@ -152,11 +152,10 @@ def tile_qa_cnn_t_kernel(tc, question, answer, W, b, out_0, out_1):
             g32 = grouped[:].bitcast(F32).rearrange("p b (r l u) -> p b r l u", r=2, u=2)
             for k in range(pairs):
                 src = turned[k][:].rearrange("p r u (b l) -> p b r l u", b=2)
-                for j in range(2):
-                    if on_scalar:
-                        nc.scalar.copy(out=g32[:, 2 * k + j], in_=src[:, j])
-                    else:
-                        nc.vector.tensor_copy(out=g32[:, 2 * k + j], in_=src[:, j])
+                if on_scalar:
+                    nc.scalar.copy(out=g32[:, 2 * k : 2 * k + 2], in_=src)
+                else:
+                    nc.vector.tensor_copy(out=g32[:, 2 * k : 2 * k + 2], in_=src)
             return grouped
 
         def quant(unit, grouped):

@@ -13,14 +13,12 @@ U8 = mybir.dt.uint8
 FP8X4 = mybir.dt.float8_e4m3fn_x4
 IDENTITY = mybir.ActivationFunctionType.Identity
 ADD = mybir.AluOpType.add
-MULT = mybir.AluOpType.mult
 
 P = 128
 L = 64
 WIDE = 4 * L
 KIND = {"a": (6, 2, 64), "q": (3, 1, 16)}
-PLAIN_PARTS = {1: ((0, 96),), 3: ((32, 64), (64, 128))}
-SHIFTED_PARTS = {1: ((96, 128),), 3: ((0, 32),)}
+SHIFTED = {1: (96, 128), 3: (0, 32)}
 NEIGHBOUR = {1: -L, 3: L}
 SLOT = {1: 0, 3: 1}
 VEC_BANKS = {"a": (), "q": ()}
@@ -46,15 +44,10 @@ def tile_qa_cnn_t_kernel(tc, question, answer, W, b, out_0, out_1):
         xq = []
         for n in range(3):
             xq.append(keep.tile([P, 1, 1024], BF16, name="xq%d" % n))
-        w_raw = keep.tile([P, 4, 1024], BF16, name="w_raw")
+        w_raw = keep.tile([P, 1024], BF16, name="w_raw")
         b_bf = keep.tile([P, 2], BF16, name="b_bf")
+        nc.sync.dma_start(out=w_raw[:], in_=w_rows)
         nc.sync.dma_start(out=xq[0][:], in_=q_rows[0])
-        nc.sync.dma_start(out=w_raw[:, 2, :], in_=w_rows)
-        for s in (3, 1, 0):
-            rot = 32 * ((2 - s) % 4)
-            eng = nc.scalar if s == 1 else nc.sync
-            eng.dma_start(out=w_raw[0 : P - rot, s, :], in_=w_rows[rot:P, :])
-            eng.dma_start(out=w_raw[P - rot : P, s, :], in_=w_rows[0:rot, :])
         nc.sync.dma_start(out=xa[0][:], in_=a_rows[0])
         with nc.allow_non_contiguous_dma(reason="256 bias values, two to a partition"):
             nc.sync.dma_start(out=b_bf[:], in_=b.rearrange("(c h) -> c h", h=2))
@@ -64,10 +57,10 @@ def tile_qa_cnn_t_kernel(tc, question, answer, W, b, out_0, out_1):
             nc.sync.dma_start(out=xa[n][:], in_=a_rows[n])
         nc.sync.dma_start(out=xq[2][:], in_=q_rows[2])
 
-        wa = keep.tile([P, 2, 256], U32, name="wa", align_bytes=64)
         wb = keep.tile([P, 2, 256], U32, name="wb", align_bytes=64)
         ident = keep.tile([P, P], F32, name="ident")
         make_identity(nc, ident[:])
+        turner = keep.tile([P, 2 * P], BF16, name="turner")
         warm = keep.tile([P, 1], F32, name="warm")
         nc.vector.memset(warm[:], 0.0)
         nc.scalar.activation(out=warm[:], in_=warm[:], func=IDENTITY, bias=0.0, scale=1.0)
@@ -81,7 +74,7 @@ def tile_qa_cnn_t_kernel(tc, question, answer, W, b, out_0, out_1):
         def in_lanes(ap, kind):
             return ap.rearrange("p (b k q l) -> p b k q l", k=4, l=KIND[kind][2], q=L // KIND[kind][2])
 
-        for t in (s_q, wa, wb, s_a):
+        for t in (s_q, wb, s_a):
             nc.gpsimd.memset(t[:].bitcast(I32), 0)
         for kind in ("q", "a"):
             v = in_lanes(store_of[kind][0][:].bitcast(I32), kind)
@@ -89,22 +82,32 @@ def tile_qa_cnn_t_kernel(tc, question, answer, W, b, out_0, out_1):
             nc.vector.memset(v[:, :, 0, :, 0:1], 0)
             nc.vector.memset(v[:, :, 3, :, last : last + 1], 0)
 
+        for half in range(2):
+            nc.vector.tensor_copy(out=turner[:, P * half : P * half + P], in_=ident[:])
         w_grp = keep.tile([P, 4, 256, 4], BF16, name="w_grp", align_bytes=64)
         wq = keep.tile([P, 4, 256], U32, name="wq", align_bytes=64)
         wqs = keep.tile([P, 4, 256], U8, name="wqs", align_bytes=64)
-        bias = keep.tile([P, 2], F32, name="bias")
 
-        def regroup_w(s, on):
-            src = w_raw[:, s, :].rearrange("p (t m h) -> p h m t", t=4, h=2)
-            dst = w_grp[:, s].rearrange("p (h m) t -> p h m t", h=2)
-            if on == "v":
-                nc.vector.tensor_copy(out=dst, in_=src)
-            elif on == "s":
-                nc.scalar.copy(out=dst, in_=src)
-            else:
-                nc.gpsimd.tensor_scalar(
-                    out=dst, in0=src, scalar1=1.0, scalar2=0.0, op0=MULT, op1=ADD
+        def new_bank():
+            acc = mm_ps.tile([P, 4, P], F32, tag="mm")
+            return acc
+
+        w_cols = w_raw[:].rearrange("p (t m h) -> p h t m", t=4, h=2)
+
+        def rotate_w(s):
+            rot = 32 * ((2 - s) % 4)
+            acc = mm_ps.tile([P, 2, 4, P], BF16, tag="mm")
+            for h in range(2):
+                nc.tensor.matmul(
+                    out=acc[:, h], lhsT=turner[:, rot : rot + P], rhs=w_cols[:, h], start=True, stop=True
                 )
+            return acc
+
+        def regroup_w(s, src):
+            nc.scalar.copy(
+                out=w_grp[:, s].rearrange("p (h m) t -> p h m t", h=2),
+                in_=src[:].rearrange("p h t m -> p h m t"),
+            )
 
         def quant_w(s):
             nc.vector.quantize_mx(
@@ -114,10 +117,10 @@ def tile_qa_cnn_t_kernel(tc, question, answer, W, b, out_0, out_1):
             )
 
         def split_w(s):
-            whole = wq[:, s, :].bitcast(I32)
-            for dst, parts in ((wa, PLAIN_PARTS[s]), (wb, SHIFTED_PARTS[s])):
-                for lo, hi in parts:
-                    nc.vector.tensor_copy(out=dst[:, SLOT[s], :].bitcast(I32)[lo:hi], in_=whole[lo:hi])
+            lo, hi = SHIFTED[s]
+            whole = wq[lo:hi, s, :].bitcast(I32)
+            nc.vector.tensor_copy(out=wb[lo:hi, SLOT[s], :].bitcast(I32), in_=whole)
+            nc.gpsimd.memset(whole, 0)
 
         def pairs_of(unit):
             return KIND[unit[0]][1]
@@ -189,10 +192,6 @@ def tile_qa_cnn_t_kernel(tc, question, answer, W, b, out_0, out_1):
                 for lo, hi, at in ((64, 128, 0), (0, 64, L // each)):
                     nc.vector.tensor_copy(out=d[lo:hi], in_=v[lo:hi, :, at : at + P // each])
 
-        def new_bank():
-            acc = mm_ps.tile([P, 4, P], F32, tag="mm")
-            return acc
-
         def multiply(unit, i, h, acc, which):
             codes, planes = store_of[unit[0]]
             at = WIDE * blocks_of(unit)[i] + L
@@ -215,7 +214,7 @@ def tile_qa_cnn_t_kernel(tc, question, answer, W, b, out_0, out_1):
                 elif s == 0:
                     one(s, wq[:, s, cols], moved[unit][0], moved[unit][1], P * i, True, True)
                 else:
-                    one(s, wa[:, SLOT[s], cols], codes, planes, at, True, False)
+                    one(s, wq[:, s, cols], codes, planes, at, True, False)
                     one(s, wb[:, SLOT[s], cols], codes, planes, at + NEIGHBOUR[s], False, True)
 
         def empty(unit, h, acc, on_vector, o):
@@ -227,11 +226,11 @@ def tile_qa_cnn_t_kernel(tc, question, answer, W, b, out_0, out_1):
                 a_view = acc[:].rearrange("c s (r b l) -> c b l r s", r=2, b=4)
             if on_vector:
                 nc.vector.tensor_scalar(
-                    out=o_view, in0=a_view, scalar1=bias[:, h : h + 1], scalar2=None, op0=ADD
+                    out=o_view, in0=a_view, scalar1=b_bf[:, h : h + 1], scalar2=None, op0=ADD
                 )
             else:
                 nc.scalar.activation(
-                    out=o_view, in_=a_view, func=IDENTITY, bias=bias[:, h : h + 1], scale=1.0
+                    out=o_view, in_=a_view, func=IDENTITY, bias=b_bf[:, h : h + 1], scale=1.0
                 )
 
         def out_tile():
@@ -261,22 +260,26 @@ def tile_qa_cnn_t_kernel(tc, question, answer, W, b, out_0, out_1):
 
         units = [("q", 0), ("a", 0), ("a", 1), ("q", 1), ("a", 2), ("a", 3), ("a", 4), ("a", 5), ("q", 2)]
 
+        w3 = rotate_w(3)
         t0 = turn(units[0])
-        regroup_w(2, "v")
-        g0 = group(units[0], t0, on_scalar=True)
-        regroup_w(1, "g")
+        w1 = rotate_w(1)
+        w0 = rotate_w(0)
+        nc.vector.tensor_copy(
+            out=w_grp[:, 2].rearrange("p (h m) t -> p h m t", h=2), in_=w_cols.rearrange("p h t m -> p h m t")
+        )
         quant_w(2)
-        regroup_w(3, "s")
-        quant(units[0], g0)
-        halo(units[0])
-        move(units[0])
+        regroup_w(3, w3)
+        g0 = group(units[0], t0, on_scalar=True)
+        regroup_w(1, w1)
+        regroup_w(0, w0)
         quant_w(3)
+        quant(units[0], g0)
         split_w(3)
         quant_w(1)
+        halo(units[0])
         split_w(1)
-        regroup_w(0, "v")
         quant_w(0)
-        nc.vector.tensor_copy(out=bias[:], in_=b_bf[:])
+        move(units[0])
         head = [(i, h, new_bank()) for i in range(2) for h in range(2)]
         for i, h, acc in head:
             multiply(units[0], i, h, acc, (2,))

from contextlib import ExitStack

import concourse.mybir as mybir
from concourse.masks import make_identity

FLOPS = 2 * 24 * (128 + 512) * 512 * 256

F32 = mybir.dt.float32
BF16 = mybir.dt.bfloat16
I32 = mybir.dt.int32
U32 = mybir.dt.uint32
U8 = mybir.dt.uint8
FP8X4 = mybir.dt.float8_e4m3fn_x4
IDENTITY = mybir.ActivationFunctionType.Identity
ADD = mybir.AluOpType.add

P = 128
L = 64
WIDE = 4 * L
KIND = {"a": (6, 2, 64), "q": (3, 1, 16)}
SHIFTED = {1: (96, 128), 3: (0, 32)}
NEIGHBOUR = {1: -L, 3: L}
SLOT = {1: 0, 3: 1}
VEC_BANKS = {"a": (), "q": ()}


def tile_qa_cnn_t_kernel(tc, question, answer, W, b, out_0, out_1):
    nc = tc.nc
    with ExitStack() as ctx:
        keep = ctx.enter_context(tc.tile_pool(name="keep", bufs=1))
        gpool = ctx.enter_context(tc.tile_pool(name="grouped", bufs=3))
        mpool = ctx.enter_context(tc.tile_pool(name="moved", bufs=3))
        opool = ctx.enter_context(tc.tile_pool(name="outs", bufs=8))
        tp_ps = ctx.enter_context(tc.psum_pool(name="tp", bufs=2))
        mm_ps = ctx.enter_context(tc.psum_pool(name="mm", bufs=6))
        ctx.enter_context(tc.manual_schedule())

        a_rows = answer.flatten_outer_dims().rearrange("(n k p g) e -> n p k (g e)", n=6, k=2, g=8)
        q_rows = question.flatten_outer_dims().rearrange("(n k p g) e -> n p k (g e)", n=3, k=1, g=8)
        w_rows = W.rearrange("(p t) c -> p (t c)", t=4)
        xa = []
        for n in range(6):
            xa.append(keep.tile([P, 2, 1024], BF16, name="xa%d" % n))
        xq = []
        for n in range(3):
            xq.append(keep.tile([P, 1, 1024], BF16, name="xq%d" % n))
        w_raw = keep.tile([P, 1024], BF16, name="w_raw")
        b_bf = keep.tile([P, 2], BF16, name="b_bf")
        nc.sync.dma_start(out=w_raw[:], in_=w_rows)
        nc.sync.dma_start(out=xq[0][:], in_=q_rows[0])
        nc.sync.dma_start(out=xa[0][:], in_=a_rows[0])
        with nc.allow_non_contiguous_dma(reason="256 bias values, two to a partition"):
            nc.sync.dma_start(out=b_bf[:], in_=b.rearrange("(c h) -> c h", h=2))
        nc.sync.dma_start(out=xa[1][:], in_=a_rows[1])
        nc.sync.dma_start(out=xq[1][:], in_=q_rows[1])
        for n in range(2, 6):
            nc.sync.dma_start(out=xa[n][:], in_=a_rows[n])
        nc.sync.dma_start(out=xq[2][:], in_=q_rows[2])

        wb = keep.tile([P, 2, 256], U32, name="wb", align_bytes=64)
        ident = keep.tile([P, P], F32, name="ident")
        make_identity(nc, ident[:])
        turner = keep.tile([P, 2 * P], BF16, name="turner")
        warm = keep.tile([P, 1], F32, name="warm")
        nc.vector.memset(warm[:], 0.0)
        nc.scalar.activation(out=warm[:], in_=warm[:], func=IDENTITY, bias=0.0, scale=1.0)

        c_a = keep.tile([P, 24 * WIDE], U32, name="c_a", align_bytes=64)
        s_a = keep.tile([P, 24 * WIDE], U8, name="s_a", align_bytes=64)
        c_q = keep.tile([P, 6 * WIDE], U32, name="c_q", align_bytes=64)
        s_q = keep.tile([P, 6 * WIDE], U8, name="s_q", align_bytes=64)
        store_of = {"a": (c_a, s_a), "q": (c_q, s_q)}

        def in_lanes(ap, kind):
            return ap.rearrange("p (b k q l) -> p b k q l", k=4, l=KIND[kind][2], q=L // KIND[kind][2])

        for t in (s_q, wb, s_a):
            nc.gpsimd.memset(t[:].bitcast(I32), 0)
        for kind in ("q", "a"):
            v = in_lanes(store_of[kind][0][:].bitcast(I32), kind)
            last = KIND[kind][2] - 1
            nc.vector.memset(v[:, :, 0, :, 0:1], 0)
            nc.vector.memset(v[:, :, 3, :, last : last + 1], 0)

        for half in range(2):
            nc.vector.tensor_copy(out=turner[:, P * half : P * half + P], in_=ident[:])
        w_grp = keep.tile([P, 4, 256, 4], BF16, name="w_grp", align_bytes=64)
        wq = keep.tile([P, 4, 256], U32, name="wq", align_bytes=64)
        wqs = keep.tile([P, 4, 256], U8, name="wqs", align_bytes=64)

        def new_bank():
            acc = mm_ps.tile([P, 4, P], F32, tag="mm")
            return acc

        w_cols = w_raw[:].rearrange("p (t m h) -> p h t m", t=4, h=2)

        def rotate_w(s):
            rot = 32 * ((2 - s) % 4)
            acc = mm_ps.tile([P, 2, 4, P], BF16, tag="mm")
            for h in range(2):
                nc.tensor.matmul(
                    out=acc[:, h], lhsT=turner[:, rot : rot + P], rhs=w_cols[:, h], start=True, stop=True
                )
            return acc

        def regroup_w(s, src):
            nc.scalar.copy(
                out=w_grp[:, s].rearrange("p (h m) t -> p h m t", h=2),
                in_=src[:].rearrange("p h t m -> p h m t"),
            )

        def quant_w(s):
            nc.vector.quantize_mx(
                out=wq[:, s, :].bitcast(FP8X4),
                scales=wqs[:, s, :],
                in_=w_grp[:, s].rearrange("p c t -> p (c t)"),
            )

        def split_w(s):
            lo, hi = SHIFTED[s]
            whole = wq[lo:hi, s, :].bitcast(I32)
            nc.vector.tensor_copy(out=wb[lo:hi, SLOT[s], :].bitcast(I32), in_=whole)
            nc.gpsimd.memset(whole, 0)

        def pairs_of(unit):
            return KIND[unit[0]][1]

        def blocks_of(unit):
            first = 2 * pairs_of(unit) * unit[1]
            return range(first, first + 2 * pairs_of(unit))

        def span(unit):
            blocks = blocks_of(unit)
            return slice(WIDE * blocks[0], WIDE * (blocks[0] + len(blocks)))

        def turn(unit):
            x = (xa if unit[0] == "a" else xq)[unit[1]]
            xw = x[:].bitcast(F32)
            turned = []
            for k in range(pairs_of(unit)):
                tp = tp_ps.tile([P, 2, 2, P], F32, tag="tp")
                turned.append(tp)
                for r in range(2):
                    for u in range(2):
                        nc.tensor.transpose(
                            tp[:, r, u, :],
                            xw[:, k, 256 * r : 256 * r + 256].rearrange("p (m u) -> p u m", u=2)[:, u, :],
                            ident[:],
                        )
            return turned

        def group(unit, turned, on_scalar=False):
            pairs = pairs_of(unit)
            grouped = gpool.tile([P, pairs * 2, 512], BF16, tag="g" + unit[0], align_bytes=64)
            g32 = grouped[:].bitcast(F32).rearrange("p b (r l u) -> p b r l u", r=2, u=2)
            for k in range(pairs):
                src = turned[k][:].rearrange("p r u (b l) -> p b r l u", b=2)
                if on_scalar:
                    nc.scalar.copy(out=g32[:, 2 * k : 2 * k + 2], in_=src)
                else:
                    nc.vector.tensor_copy(out=g32[:, 2 * k : 2 * k + 2], in_=src)
            return grouped

        def quant(unit, grouped):
            codes, planes = store_of[unit[0]]
            for i, blk in enumerate(blocks_of(unit)):
                lo = WIDE * blk + L
                nc.vector.quantize_mx(
                    out=codes[:, lo : lo + P].bitcast(FP8X4),
                    scales=planes[:, lo : lo + P],
                    in_=grouped[:, i, :],
                )

        def halo(unit):
            codes, planes = store_of[unit[0]]
            last = KIND[unit[0]][2] - 1
            for ap in (codes[:, span(unit)].bitcast(I32), planes[:, span(unit)]):
                v = in_lanes(ap, unit[0])
                nc.vector.tensor_copy(out=v[:, :, 0, :, 1 : last + 1], in_=v[:, :, 2, :, 0:last])
                nc.vector.tensor_copy(out=v[:, :, 3, :, 0:last], in_=v[:, :, 1, :, 1 : last + 1])

        moved = {}

        def move(unit):
            n = len(blocks_of(unit))
            mc = mpool.tile([P, n * P], U32, tag="mc" + unit[0], align_bytes=64)
            ms = mpool.tile([P, n * P], U8, tag="ms" + unit[0], align_bytes=64)
            moved[unit] = (mc, ms)
            for src, dst, each in ((store_of[unit[0]][0], mc, 1), (store_of[unit[0]][1], ms, 4)):
                v = src[:, span(unit)].bitcast(I32).rearrange("p (b w) -> p b w", w=WIDE // each)
                d = dst[:].bitcast(I32).rearrange("p (b w) -> p b w", w=P // each)
                for lo, hi, at in ((64, 128, 0), (0, 64, L // each)):
                    nc.vector.tensor_copy(out=d[lo:hi], in_=v[lo:hi, :, at : at + P // each])

        def multiply(unit, i, h, acc, which):
            codes, planes = store_of[unit[0]]
            at = WIDE * blocks_of(unit)[i] + L
            cols = slice(P * h, P * h + P)

            def one(s, weights, xc, xs, col, start, stop):
                nc.tensor.matmul_mx(
                    out=acc[:, s, :],
                    lhsT=weights.bitcast(FP8X4),
                    lhsT_scale=wqs[:, s, cols],
                    rhs=xc[:, col : col + P].bitcast(FP8X4),
                    rhs_scale=xs[:, col : col + P],
                    start=start,
                    stop=stop,
                )

            for s in which:
                if s == 2:
                    one(s, wq[:, s, cols], codes, planes, at, True, True)
                elif s == 0:
                    one(s, wq[:, s, cols], moved[unit][0], moved[unit][1], P * i, True, True)
                else:
                    one(s, wq[:, s, cols], codes, planes, at, True, False)
                    one(s, wb[:, SLOT[s], cols], codes, planes, at + NEIGHBOUR[s], False, True)

        def empty(unit, h, acc, on_vector, o):
            if unit[0] == "a":
                o_view = o.rearrange("c (h l r s) -> c h r l s", h=2, r=2, s=4)[:, h]
                a_view = acc[:].rearrange("c s (r l) -> c r l s", r=2)
            else:
                o_view = o.rearrange("c (b h l r s) -> c h b l r s", b=4, h=2, r=2, s=4)[:, h]
                a_view = acc[:].rearrange("c s (r b l) -> c b l r s", r=2, b=4)
            if on_vector:
                nc.vector.tensor_scalar(
                    out=o_view, in0=a_view, scalar1=b_bf[:, h : h + 1], scalar2=None, op0=ADD
                )
            else:
                nc.scalar.activation(
                    out=o_view, in_=a_view, func=IDENTITY, bias=b_bf[:, h : h + 1], scale=1.0
                )

        def out_tile():
            o = opool.tile([P, 1024], F32, tag="o")
            return o

        def store(unit, i, o):
            blk = blocks_of(unit)[i]
            if unit[0] == "a":
                nc.sync.dma_start(out=out_1[blk].rearrange("(c h) i -> c (h i)", h=2), in_=o[:])
            else:
                nc.sync.dma_start(
                    out=out_0[4 * blk : 4 * blk + 4].rearrange("b (c h) i -> c b (h i)", h=2),
                    in_=o[:].rearrange("c (b f) -> c b f", b=4),
                )

        def run(unit, after):
            for i in range(len(blocks_of(unit))):
                o = out_tile()
                for h in range(2):
                    acc = new_bank()
                    multiply(unit, i, h, acc, (2, 3, 1, 0))
                    empty(unit, h, acc, 2 * i + h in VEC_BANKS[unit[0]], o[:])
                    if 2 * i + h in after:
                        after[2 * i + h]()
                store(unit, i, o)

        units = [("q", 0), ("a", 0), ("a", 1), ("q", 1), ("a", 2), ("a", 3), ("a", 4), ("a", 5), ("q", 2)]

        w3 = rotate_w(3)
        t0 = turn(units[0])
        w1 = rotate_w(1)
        w0 = rotate_w(0)
        nc.vector.tensor_copy(
            out=w_grp[:, 2].rearrange("p (h m) t -> p h m t", h=2), in_=w_cols.rearrange("p h t m -> p h m t")
        )
        quant_w(2)
        regroup_w(3, w3)
        g0 = group(units[0], t0, on_scalar=True)
        regroup_w(1, w1)
        regroup_w(0, w0)
        quant_w(3)
        quant(units[0], g0)
        split_w(3)
        quant_w(1)
        halo(units[0])
        split_w(1)
        quant_w(0)
        move(units[0])
        head = [(i, h, new_bank()) for i in range(2) for h in range(2)]
        for i, h, acc in head:
            multiply(units[0], i, h, acc, (2,))
        t1 = turn(units[1])
        g1 = group(units[1], t1, on_scalar=True)
        for s in (3, 1, 0):
            for i, h, acc in head:
                multiply(units[0], i, h, acc, (s,))
        quant(units[1], g1)
        halo(units[1])
        move(units[1])
        t2 = turn(units[2])
        for i in range(2):
            o = out_tile()
            for h in range(2):
                empty(units[0], h, head[2 * i + h][2], 2 * i + h in VEC_BANKS["q"], o[:])
            store(units[0], i, o)
        g2 = group(units[2], t2)
        quant(units[2], g2)
        halo(units[2])
        move(units[2])

        def hooks(i):
            if i + 2 >= len(units):
                return {}
            ahead = units[i + 2]
            half = 4 if units[i][0] == "a" else 2
            held = {}

            def first():
                held["g"] = group(ahead, turn(ahead))

            def third():
                halo(ahead)
                move(ahead)

            return {half - 1: first, half: lambda: quant(ahead, held["g"]), half + 1: third}

        for i in range(1, len(units)):
            run(units[i], hooks(i))
